import numpy as np
import ml_dtypes


def mxq(x, axis, fmt="e4m3"):
    dtype, down = {"e4m3": (ml_dtypes.float8_e4m3fn, 7), "e5m2": (ml_dtypes.float8_e5m2, 14)}[fmt]
    v = np.moveaxis(np.asarray(x, np.float32).astype(ml_dtypes.bfloat16).astype(np.float64), axis, -1)
    blocks = v.reshape(v.shape[:-1] + (-1, 32))
    amax = np.abs(blocks).max(-1, keepdims=True)
    byte = np.maximum(np.where(amax > 0, np.frexp(amax)[1] - 1 + 127, 0) - down, 1)
    scale = np.exp2(byte - 127.0)
    codes = (blocks / scale).astype(np.float32).astype(dtype).astype(np.float64)
    return np.moveaxis((codes * scale).reshape(v.shape), -1, axis)


WIDE = False


def mx_kscale(k):
    if not WIDE:
        return np.ones(k)
    levels = np.array([10, -10, 5, -5, 0])
    a = np.random.permutation(np.resize(levels, k // 512 * 4)).reshape(k // 512, 4)
    idx = np.arange(k)
    return np.exp2(a[idx // 512, idx % 128 // 32])


BF16 = ml_dtypes.bfloat16


def bf(x):
    return np.asarray(x, np.float32).astype(BF16)


def f64(x):
    return np.asarray(x).astype(np.float64)


B, C, O, ROWS, COLS, KH, KW = 1024, 64, 128, 4, 4, 4, 4
H, W, K = ROWS + KH - 1, COLS + KW - 1, C * KH * KW


def setup_inputs():
    sc = mx_kscale(K)[::KH * KW]
    return {"x": bf(np.random.standard_normal((B, C, H, W)) * sc[None, :, None, None]),
            "weight": bf(np.random.standard_normal((ROWS, COLS, O, C, KH, KW)) / np.sqrt(K) / sc[None, None, None, :, None, None])}


def reference(x, weight):
    x, weight = f64(x), f64(weight)
    rows, cols, o, c, kh, kw = weight.shape
    b = x.shape[0]
    patches = np.stack(
        [np.stack([x[:, :, u:u + rows, v:v + cols] for v in range(kw)], axis=2)
         for u in range(kh)], axis=2)
    p = patches.transpose(4, 5, 0, 1, 2, 3).reshape(rows * cols, b, c * kh * kw)
    w = weight.reshape(rows * cols, o, c * kh * kw)
    y = mxq(p, 2, "e4m3") @ mxq(w, 2, "e4m3").transpose(0, 2, 1)
    return y.reshape(rows, cols, b, o).transpose(2, 3, 0, 1)

@@ -1,0 +1,100 @@
+import concourse.mybir as mybir
+from concourse.masks import make_identity
+
+F32 = mybir.dt.float32
+BF16 = mybir.dt.bfloat16
+U32 = mybir.dt.uint32
+U8 = mybir.dt.uint8
+FP8X4 = mybir.dt.float8_e4m3fn_x4
+
+P = 128
+B, C, O, ROWS, COLS, KH, KW, H, W = 1024, 64, 128, 4, 4, 4, 4, 7, 7
+FLOPS = 2 * ROWS * COLS * B * O * C * KH * KW
+NBT = B // P
+NHB = 5
+
+
+def tile_localconvolution_t_kernel(tc, x, weight, out):
+    nc = tc.nc
+    with tc.tile_pool(name="const", bufs=1) as const, \
+            tc.tile_pool(name="xin", bufs=3) as xin, \
+            tc.tile_pool(name="stg", bufs=2) as stg, \
+            tc.tile_pool(name="grp", bufs=2) as grp, \
+            tc.tile_pool(name="cod", bufs=4) as cod, \
+            tc.tile_pool(name="res", bufs=2) as res, \
+            tc.tile_pool(name="wld", bufs=2) as wld, \
+            tc.psum_pool(name="pt", bufs=4) as pt, \
+            tc.psum_pool(name="pa", bufs=4) as pa:
+        ident = const.tile([P, P], F32)
+        make_identity(nc, ident[:])
+        wc = const.tile([P, ROWS * COLS * 2 * O], U32, align_bytes=64)
+        ws = const.tile([P, ROWS * COLS * 2 * O], U8, align_bytes=64)
+
+        def load_x(bt):
+            xt = xin.tile([P, C * H * W], BF16, name="xt")
+            nc.sync.dma_start(out=xt[:], in_=x[bt * P:(bt + 1) * P].rearrange("b c h w -> b (c h w)"))
+            return xt
+
+        xts = {0: load_x(0)}
+
+        for i in range(ROWS):
+            wraw = wld.tile([P, COLS * 1024], BF16, name="wraw")
+            nc.sync.dma_start(
+                out=wraw[:].rearrange("o (j k) -> o j k", j=COLS),
+                in_=weight[i].rearrange("j o c u v -> o j (c u v)"))
+            wst = wld.tile([P, COLS * 1024], BF16, name="wst")
+            wg = wld.tile([P, COLS * 1024], BF16, name="wg", align_bytes=64)
+            wraw32 = wraw[:].bitcast(F32)
+            wst32 = wst[:].bitcast(F32)
+            wg32 = wg[:].bitcast(F32).rearrange("p (j q o r) -> p j q o r", j=COLS, q=2, o=O, r=2)
+            for j in range(COLS):
+                nc.vector.tensor_copy(
+                    out=wst32[:, j * 512:(j + 1) * 512].rearrange("p (u b a w) -> p u b a w", u=4, b=8, a=8, w=2),
+                    in_=wraw32[:, j * 512:(j + 1) * 512].rearrange("p (a b u w) -> p u b a w", a=8, b=8, u=4, w=2))
+                pw = pt.tile([P, 4, P], F32, name="pw", tag="pt")
+                for u in range(KH):
+                    nc.tensor.transpose(pw[:, u, :], wst32[:, (j * 4 + u) * P:(j * 4 + u + 1) * P], ident[:])
+                nc.scalar.copy(out=wg32[:, j], in_=pw[:].rearrange("p (r q) o -> p q o r", r=2, q=2))
+            nc.vector.quantize_mx(
+                out=wc[:, i * 1024:(i + 1) * 1024].bitcast(FP8X4),
+                scales=ws[:, i * 1024:(i + 1) * 1024],
+                in_=wg[:])
+
+        for bt in range(NBT):
+            if bt + 1 < NBT:
+                xts[bt + 1] = load_x(bt + 1)
+            xt = xts[bt]
+            st = stg.tile([P, COLS * H * 256], BF16, name="st")
+            st32 = st[:].bitcast(F32)
+            g = grp.tile([P, NHB * COLS * P * 4], BF16, name="g", align_bytes=64)
+            g32 = g[:].bitcast(F32).rearrange("p (h j b r) -> p h j b r", h=NHB, j=COLS, b=P, r=2)
+            xv = xt[:].rearrange("p (a b h w) -> p h b a w", a=8, b=8, h=H, w=W)
+            for j in range(COLS):
+                nc.vector.tensor_copy(
+                    out=st[:, j * H * 256:(j + 1) * H * 256].rearrange("p (h b a v) -> p h b a v", h=H, b=8, a=8, v=4),
+                    in_=xv[:, :, :, :, j:j + 4])
+                for par in range(2):
+                    rows = list(range(par, H, 2))
+                    pe = pt.tile([P, 4, P], F32, name="pe", tag="pt")
+                    for s, h in enumerate(rows):
+                        nc.tensor.transpose(pe[:, s, :], st32[:, (j * H + h) * P:(j * H + h + 1) * P], ident[:])
+                    for s in range(len(rows) - 1):
+                        nc.scalar.copy(out=g32[:, rows[s], j], in_=pe[:, s:s + 2, :].rearrange("p r b -> p b r"))
+            stage = res.tile([P, O * ROWS * COLS], F32, name="stage")
+            stv = stage[:].rearrange("p (o i j) -> p o i j", o=O, i=ROWS, j=COLS)
+            for i in range(ROWS):
+                pc = cod.tile([P, 1024], U32, name="pc", align_bytes=64)
+                psc = cod.tile([P, 1024], U8, name="psc", align_bytes=64)
+                nc.vector.quantize_mx(out=pc[:].bitcast(FP8X4), scales=psc[:], in_=g[:, i * 2048:i * 2048 + 4096])
+                acc = pa.tile([P, COLS * O], F32, name="acc")
+                for j in range(COLS):
+                    for q in range(2):
+                        lo = q * 512 + j * P
+                        wo = ((i * COLS + j) * 2 + q) * O
+                        nc.tensor.matmul_mx(
+                            out=acc[:, j * O:(j + 1) * O],
+                            lhsT=pc[:, lo:lo + P].bitcast(FP8X4), lhsT_scale=psc[:, lo:lo + P],
+                            rhs=wc[:, wo:wo + O].bitcast(FP8X4), rhs_scale=ws[:, wo:wo + O],
+                            start=(q == 0), stop=(q == 1))
+                nc.scalar.copy(out=stv[:, :, i, :], in_=acc[:].rearrange("p (j o) -> p o j", j=COLS))
+            nc.sync.dma_start(out=out[bt * P:(bt + 1) * P].rearrange("b o i j -> b (o i j)"), in_=stage[:])

@@ -12,6 +12,8 @@ B, C, O, ROWS, COLS, KH, KW, H, W = 1024, 64, 128, 4, 4, 4, 4, 7, 7
 FLOPS = 2 * ROWS * COLS * B * O * C * KH * KW
 NBT = B // P
 NHB = 5
+XPAD = 3200
+NW = C * H * W // 2
 
 
 def tile_localconvolution_t_kernel(tc, x, weight, out):
@@ -31,9 +33,12 @@ def tile_localconvolution_t_kernel(tc, x, weight, out):
         ws = const.tile([P, ROWS * COLS * 2 * O], U8, align_bytes=64)
 
         def load_x(bt):
-            xt = xin.tile([P, C * H * W], BF16, name="xt")
-            nc.sync.dma_start(out=xt[:], in_=x[bt * P:(bt + 1) * P].rearrange("b c h w -> b (c h w)"))
-            return xt
+            rows = x[bt * P:(bt + 1) * P].rearrange("b c h w -> b (c h w)")
+            x0 = xin.tile([P, XPAD], BF16, name="x0")
+            nc.sync.dma_start(out=x0[:, 0:C * H * W], in_=rows)
+            x1 = xin.tile([P, XPAD], BF16, name="x1")
+            nc.sync.dma_start(out=x1[:, 0:C * H * W - 1], in_=rows[:, 1:C * H * W])
+            return (x0, x1)
 
         xts = {0: load_x(0)}
 
@@ -64,20 +69,27 @@ def tile_localconvolution_t_kernel(tc, x, weight, out):
             if bt + 1 < NBT:
                 xts[bt + 1] = load_x(bt + 1)
             xt = xts[bt]
-            st = stg.tile([P, COLS * H * 256], BF16, name="st")
+            st = stg.tile([P, COLS * 8 * 256], BF16, name="st")
             st32 = st[:].bitcast(F32)
             g = grp.tile([P, NHB * COLS * P * 4], BF16, name="g", align_bytes=64)
             g32 = g[:].bitcast(F32).rearrange("p (h j b r) -> p h j b r", h=NHB, j=COLS, b=P, r=2)
-            xv = xt[:].rearrange("p (a b h w) -> p h b a w", a=8, b=8, h=H, w=W)
+            xw = (xt[0][:].bitcast(F32), xt[1][:].bitcast(F32))
             for j in range(COLS):
-                nc.vector.tensor_copy(
-                    out=st[:, j * H * 256:(j + 1) * H * 256].rearrange("p (h b a v) -> p h b a v", h=H, b=8, a=8, v=4),
-                    in_=xv[:, :, :, :, j:j + 4])
+                stj = st32[:, j * 1024:(j + 1) * 1024].rearrange(
+                    "p (s x k e a r) -> p x e s k a r", s=4, x=2, k=4, e=2, a=8, r=2)
+                for e in range(2):
+                    for hp in range(2):
+                        nh = 4 - hp
+                        par = (e + hp + j) % 2
+                        off = (49 * e + 7 * hp + j - par) // 2
+                        src = xw[par][:, off:off + NW].rearrange(
+                            "p (a k s r) -> p s k a r", a=8, k=4, s=7, r=7)
+                        nc.vector.tensor_copy(out=stj[:, hp, e, 0:nh], in_=src[:, 0:nh, :, :, 0:2])
                 for par in range(2):
                     rows = list(range(par, H, 2))
                     pe = pt.tile([P, 4, P], F32, name="pe", tag="pt")
                     for s, h in enumerate(rows):
-                        nc.tensor.transpose(pe[:, s, :], st32[:, (j * H + h) * P:(j * H + h + 1) * P], ident[:])
+                        nc.tensor.transpose(pe[:, s, :], st32[:, (j * 8 + h) * P:(j * 8 + h + 1) * P], ident[:])
                     for s in range(len(rows) - 1):
                         nc.scalar.copy(out=g32[:, rows[s], j], in_=pe[:, s:s + 2, :].rearrange("p r b -> p b r"))
             stage = res.tile([P, O * ROWS * COLS], F32, name="stage")

@@ -53,9 +53,12 @@ def tile_localconvolution_t_kernel(tc, x, weight, out):
             wst32 = wst[:].bitcast(F32)
             wg32 = wg[:].bitcast(F32).rearrange("p (j q o r) -> p j q o r", j=COLS, q=2, o=O, r=2)
             for j in range(COLS):
-                nc.vector.tensor_copy(
-                    out=wst32[:, j * 512:(j + 1) * 512].rearrange("p (u b a w) -> p u b a w", u=4, b=8, a=8, w=2),
-                    in_=wraw32[:, j * 512:(j + 1) * 512].rearrange("p (a b u w) -> p u b a w", a=8, b=8, u=4, w=2))
+                wsrc = wraw32[:, j * 512:(j + 1) * 512].rearrange(
+                    "p (g a b h m) -> p h g b a m", g=2, a=4, b=8, h=2, m=4)
+                wdst = wst32[:, j * 512:(j + 1) * 512].rearrange(
+                    "p (h m g b a) -> p h g b a m", h=2, m=4, g=2, b=8, a=4)
+                for uh in range(2):
+                    nc.vector.tensor_copy(out=wdst[:, uh], in_=wsrc[:, uh])
                 pw = pt.tile([P, 4, P], F32, name="pw", tag="pt")
                 for u in range(KH):
                     nc.tensor.transpose(pw[:, u, :], wst32[:, (j * 4 + u) * P:(j * 4 + u + 1) * P], ident[:])
@@ -69,31 +72,33 @@ def tile_localconvolution_t_kernel(tc, x, weight, out):
             if bt + 1 < NBT:
                 xts[bt + 1] = load_x(bt + 1)
             xt = xts[bt]
-            st = stg.tile([P, COLS * 8 * 256], BF16, name="st")
+            st = stg.tile([P, 8 * 2 * 3 * 128], BF16, name="st")
             st32 = st[:].bitcast(F32)
             g = grp.tile([P, NHB * COLS * P * 4], BF16, name="g", align_bytes=64)
             g32 = g[:].bitcast(F32).rearrange("p (h j b r) -> p h j b r", h=NHB, j=COLS, b=P, r=2)
             xw = (xt[0][:].bitcast(F32), xt[1][:].bitcast(F32))
-            for j in range(COLS):
-                stj = st32[:, j * 1024:(j + 1) * 1024].rearrange(
-                    "p (s x k e a r) -> p x e s k a r", s=4, x=2, k=4, e=2, a=8, r=2)
-                for e in range(2):
-                    for hp in range(2):
+            stv = st32.rearrange(
+                "p (s x c w g k e a) -> p x c g e s k a w", s=4, x=2, c=2, w=3, g=2, k=4, e=2, a=4)
+            for ch in range(2):
+                for hp in range(2):
+                    for e in range(2):
                         nh = 4 - hp
-                        par = (e + hp + j) % 2
-                        off = (49 * e + 7 * hp + j - par) // 2
+                        par = (e + hp + ch) % 2
+                        off = (49 * e + 7 * hp + ch - par) // 2
                         src = xw[par][:, off:off + NW].rearrange(
-                            "p (a k s r) -> p s k a r", a=8, k=4, s=7, r=7)
-                        nc.vector.tensor_copy(out=stj[:, hp, e, 0:nh], in_=src[:, 0:nh, :, :, 0:2])
+                            "p (g a k s r) -> p g s k a r", g=2, a=4, k=4, s=7, r=7)
+                        for gg in range(2):
+                            nc.vector.tensor_copy(out=stv[:, hp, ch, gg, e, 0:nh], in_=src[:, gg, 0:nh, :, :, 0:3])
+            for j in range(COLS):
                 for par in range(2):
                     rows = list(range(par, H, 2))
                     pe = pt.tile([P, 4, P], F32, name="pe", tag="pt")
                     for s, h in enumerate(rows):
-                        nc.tensor.transpose(pe[:, s, :], st32[:, (j * 8 + h) * P:(j * 8 + h + 1) * P], ident[:])
+                        nc.tensor.transpose(pe[:, s, :], st32[:, ((h * 2 + j % 2) * 3 + j // 2) * 64:((h * 2 + j % 2) * 3 + j // 2) * 64 + P], ident[:])
                     for s in range(len(rows) - 1):
                         nc.scalar.copy(out=g32[:, rows[s], j], in_=pe[:, s:s + 2, :].rearrange("p r b -> p b r"))
             stage = res.tile([P, O * ROWS * COLS], F32, name="stage")
-            stv = stage[:].rearrange("p (o i j) -> p o i j", o=O, i=ROWS, j=COLS)
+            sgv = stage[:].rearrange("p (o i j) -> p o i j", o=O, i=ROWS, j=COLS)
             for i in range(ROWS):
                 pc = cod.tile([P, 1024], U32, name="pc", align_bytes=64)
                 psc = cod.tile([P, 1024], U8, name="psc", align_bytes=64)
@@ -108,5 +113,5 @@ def tile_localconvolution_t_kernel(tc, x, weight, out):
                             lhsT=pc[:, lo:lo + P].bitcast(FP8X4), lhsT_scale=psc[:, lo:lo + P],
                             rhs=wc[:, wo:wo + O].bitcast(FP8X4), rhs_scale=ws[:, wo:wo + O],
                             start=(q == 0), stop=(q == 1))
-                nc.scalar.copy(out=stv[:, :, i, :], in_=acc[:].rearrange("p (j o) -> p o j", j=COLS))
+                nc.scalar.copy(out=sgv[:, :, i, :], in_=acc[:].rearrange("p (j o) -> p o j", j=COLS))
             nc.sync.dma_start(out=out[bt * P:(bt + 1) * P].rearrange("b o i j -> b (o i j)"), in_=stage[:])

@@ -24,34 +24,38 @@ def tile_localconvolution_t_kernel(tc, x, weight, out):
             tc.tile_pool(name="grp", bufs=2) as grp, \
             tc.tile_pool(name="cod", bufs=4) as cod, \
             tc.tile_pool(name="res", bufs=2) as res, \
+            tc.tile_pool(name="wl4", bufs=4) as wl4, \
             tc.tile_pool(name="wld", bufs=2) as wld, \
             tc.psum_pool(name="pt", bufs=4) as pt, \
-            tc.psum_pool(name="pa", bufs=4) as pa:
+            tc.psum_pool(name="pa", bufs=4) as pa, \
+            tc.manual_schedule():
         ident = const.tile([P, P], F32)
         make_identity(nc, ident[:])
         wc = const.tile([P, ROWS * COLS * 2 * O], U32, align_bytes=64)
         ws = const.tile([P, ROWS * COLS * 2 * O], U8, align_bytes=64)
+        xts, sts, gs, banks, codes, accs, stages = {}, {}, {}, {}, {}, {}, {}
+        wraws, wsts, wgs, wbanks = {}, {}, {}, {}
 
-        def load_x(bt):
-            rows = x[bt * P:(bt + 1) * P].rearrange("b c h w -> b (c h w)")
+        def load_x(n):
+            rows = x[n * P:(n + 1) * P].rearrange("b c h w -> b (c h w)")
             x0 = xin.tile([P, XPAD], BF16, name="x0")
             nc.sync.dma_start(out=x0[:, 0:C * H * W], in_=rows)
             x1 = xin.tile([P, XPAD], BF16, name="x1")
             nc.sync.dma_start(out=x1[:, 0:C * H * W - 1], in_=rows[:, 1:C * H * W])
-            return (x0, x1)
+            xts[n] = (x0, x1)
 
-        xts = {0: load_x(0)}
-
-        for i in range(ROWS):
-            wraw = wld.tile([P, COLS * 1024], BF16, name="wraw")
+        def load_w(i):
+            wraw = wl4.tile([P, COLS * 1024], BF16, name="wraw")
             nc.sync.dma_start(
                 out=wraw[:].rearrange("o (j k) -> o j k", j=COLS),
                 in_=weight[i].rearrange("j o c u v -> o j (c u v)"))
+            wraws[i] = wraw
+
+        def stage_w(i):
             wst = wld.tile([P, COLS * 1024], BF16, name="wst")
-            wg = wld.tile([P, COLS * 1024], BF16, name="wg", align_bytes=64)
-            wraw32 = wraw[:].bitcast(F32)
+            wsts[i] = wst
+            wraw32 = wraws[i][:].bitcast(F32)
             wst32 = wst[:].bitcast(F32)
-            wg32 = wg[:].bitcast(F32).rearrange("p (j q o r) -> p j q o r", j=COLS, q=2, o=O, r=2)
             for j in range(COLS):
                 wsrc = wraw32[:, j * 512:(j + 1) * 512].rearrange(
                     "p (g a b h m) -> p h g b a m", g=2, a=4, b=8, h=2, m=4)
@@ -59,59 +63,131 @@ def tile_localconvolution_t_kernel(tc, x, weight, out):
                     "p (h m g b a) -> p h g b a m", h=2, m=4, g=2, b=8, a=4)
                 for uh in range(2):
                     nc.vector.tensor_copy(out=wdst[:, uh], in_=wsrc[:, uh])
+
+        def transpose_w(i):
+            wst32 = wsts[i][:].bitcast(F32)
+            for j in range(COLS):
                 pw = pt.tile([P, 4, P], F32, name="pw", tag="pt")
+                wbanks[(i, j)] = pw
                 for u in range(KH):
                     nc.tensor.transpose(pw[:, u, :], wst32[:, (j * 4 + u) * P:(j * 4 + u + 1) * P], ident[:])
-                nc.scalar.copy(out=wg32[:, j], in_=pw[:].rearrange("p (r q) o -> p q o r", r=2, q=2))
+
+        def exit_w(i):
+            wg = wld.tile([P, COLS * 1024], BF16, name="wg", align_bytes=64)
+            wgs[i] = wg
+            wg32 = wg[:].bitcast(F32).rearrange("p (j q o r) -> p j q o r", j=COLS, q=2, o=O, r=2)
+            for j in range(COLS):
+                nc.scalar.copy(out=wg32[:, j], in_=wbanks[(i, j)][:].rearrange("p (r q) o -> p q o r", r=2, q=2))
+
+        def quant_w(i):
             nc.vector.quantize_mx(
                 out=wc[:, i * 1024:(i + 1) * 1024].bitcast(FP8X4),
                 scales=ws[:, i * 1024:(i + 1) * 1024],
-                in_=wg[:])
+                in_=wgs[i][:])
 
-        for bt in range(NBT):
-            if bt + 1 < NBT:
-                xts[bt + 1] = load_x(bt + 1)
-            xt = xts[bt]
-            st = stg.tile([P, 8 * 2 * 3 * 128], BF16, name="st")
-            st32 = st[:].bitcast(F32)
-            g = grp.tile([P, NHB * COLS * P * 4], BF16, name="g", align_bytes=64)
-            g32 = g[:].bitcast(F32).rearrange("p (h j b r) -> p h j b r", h=NHB, j=COLS, b=P, r=2)
-            xw = (xt[0][:].bitcast(F32), xt[1][:].bitcast(F32))
+        def stage_x(n, ch):
+            if ch == 0:
+                sts[n] = stg.tile([P, 8 * 2 * 3 * 128], BF16, name="st")
+            st32 = sts[n][:].bitcast(F32)
+            xw = (xts[n][0][:].bitcast(F32), xts[n][1][:].bitcast(F32))
             stv = st32.rearrange(
                 "p (s x c w g k e a) -> p x c g e s k a w", s=4, x=2, c=2, w=3, g=2, k=4, e=2, a=4)
-            for ch in range(2):
-                for hp in range(2):
-                    for e in range(2):
-                        nh = 4 - hp
-                        par = (e + hp + ch) % 2
-                        off = (49 * e + 7 * hp + ch - par) // 2
-                        src = xw[par][:, off:off + NW].rearrange(
-                            "p (g a k s r) -> p g s k a r", g=2, a=4, k=4, s=7, r=7)
-                        for gg in range(2):
-                            nc.vector.tensor_copy(out=stv[:, hp, ch, gg, e, 0:nh], in_=src[:, gg, 0:nh, :, :, 0:3])
-            for j in range(COLS):
+            for hp in range(2):
+                for e in range(2):
+                    nh = 4 - hp
+                    par = (e + hp + ch) % 2
+                    off = (49 * e + 7 * hp + ch - par) // 2
+                    src = xw[par][:, off:off + NW].rearrange(
+                        "p (g a k s r) -> p g s k a r", g=2, a=4, k=4, s=7, r=7)
+                    for gg in range(2):
+                        nc.vector.tensor_copy(out=stv[:, hp, ch, gg, e, 0:nh], in_=src[:, gg, 0:nh, :, :, 0:3])
+
+        def transpose_x(n, ch):
+            st32 = sts[n][:].bitcast(F32)
+            for j in (ch, ch + 2):
                 for par in range(2):
-                    rows = list(range(par, H, 2))
                     pe = pt.tile([P, 4, P], F32, name="pe", tag="pt")
-                    for s, h in enumerate(rows):
-                        nc.tensor.transpose(pe[:, s, :], st32[:, ((h * 2 + j % 2) * 3 + j // 2) * 64:((h * 2 + j % 2) * 3 + j // 2) * 64 + P], ident[:])
-                    for s in range(len(rows) - 1):
-                        nc.scalar.copy(out=g32[:, rows[s], j], in_=pe[:, s:s + 2, :].rearrange("p r b -> p b r"))
-            stage = res.tile([P, O * ROWS * COLS], F32, name="stage")
-            sgv = stage[:].rearrange("p (o i j) -> p o i j", o=O, i=ROWS, j=COLS)
-            for i in range(ROWS):
-                pc = cod.tile([P, 1024], U32, name="pc", align_bytes=64)
-                psc = cod.tile([P, 1024], U8, name="psc", align_bytes=64)
-                nc.vector.quantize_mx(out=pc[:].bitcast(FP8X4), scales=psc[:], in_=g[:, i * 2048:i * 2048 + 4096])
-                acc = pa.tile([P, COLS * O], F32, name="acc")
-                for j in range(COLS):
-                    for q in range(2):
-                        lo = q * 512 + j * P
-                        wo = ((i * COLS + j) * 2 + q) * O
-                        nc.tensor.matmul_mx(
-                            out=acc[:, j * O:(j + 1) * O],
-                            lhsT=pc[:, lo:lo + P].bitcast(FP8X4), lhsT_scale=psc[:, lo:lo + P],
-                            rhs=wc[:, wo:wo + O].bitcast(FP8X4), rhs_scale=ws[:, wo:wo + O],
-                            start=(q == 0), stop=(q == 1))
-                nc.scalar.copy(out=sgv[:, :, i, :], in_=acc[:].rearrange("p (j o) -> p o j", j=COLS))
-            nc.sync.dma_start(out=out[bt * P:(bt + 1) * P].rearrange("b o i j -> b (o i j)"), in_=stage[:])
+                    banks[(n, j, par)] = pe
+                    for s, h in enumerate(range(par, H, 2)):
+                        lo = ((h * 2 + ch) * 3 + j // 2) * 64
+                        nc.tensor.transpose(pe[:, s, :], st32[:, lo:lo + P], ident[:])
+
+        def exit_x(n, ch):
+            if ch == 0:
+                gs[n] = grp.tile([P, NHB * COLS * P * 4], BF16, name="g", align_bytes=64)
+            g32 = gs[n][:].bitcast(F32).rearrange("p (h j b r) -> p h j b r", h=NHB, j=COLS, b=P, r=2)
+            for j in (ch, ch + 2):
+                ev = banks[(n, j, 0)]
+                od = banks[(n, j, 1)]
+                nc.scalar.copy(out=g32[:, 0:5:4, j], in_=ev[:].rearrange("p (h r) b -> p h b r", h=2, r=2))
+                nc.scalar.copy(out=g32[:, 2, j], in_=ev[:, 1:3, :].rearrange("p r b -> p b r"))
+                nc.scalar.copy(out=g32[:, 1, j], in_=od[:, 0:2, :].rearrange("p r b -> p b r"))
+                eng = nc.vector.tensor_copy if j >= 2 else nc.scalar.copy
+                eng(out=g32[:, 3, j], in_=od[:, 1:3, :].rearrange("p r b -> p b r"))
+
+        def quant_x(n, i):
+            pc = cod.tile([P, 1024], U32, name="pc", align_bytes=64)
+            psc = cod.tile([P, 1024], U8, name="psc", align_bytes=64)
+            codes[(n, i)] = (pc, psc)
+            nc.vector.quantize_mx(out=pc[:].bitcast(FP8X4), scales=psc[:], in_=gs[n][:, i * 2048:i * 2048 + 4096])
+
+        def multiply(n, i):
+            pc, psc = codes[(n, i)]
+            acc = pa.tile([P, COLS * O], F32, name="acc")
+            accs[(n, i)] = acc
+            for j in range(COLS):
+                for q in range(2):
+                    lo = q * 512 + j * P
+                    wo = ((i * COLS + j) * 2 + q) * O
+                    nc.tensor.matmul_mx(
+                        out=acc[:, j * O:(j + 1) * O],
+                        lhsT=pc[:, lo:lo + P].bitcast(FP8X4), lhsT_scale=psc[:, lo:lo + P],
+                        rhs=wc[:, wo:wo + O].bitcast(FP8X4), rhs_scale=ws[:, wo:wo + O],
+                        start=(q == 0), stop=(q == 1))
+
+        def exit_out(n, i):
+            if i == 0:
+                stages[n] = res.tile([P, O * ROWS * COLS], F32, name="stage")
+            sgv = stages[n][:].rearrange("p (o i j) -> p o i j", o=O, i=ROWS, j=COLS)
+            nc.scalar.copy(out=sgv[:, :, i, :], in_=accs[(n, i)][:].rearrange("p (j o) -> p o j", j=COLS))
+            if i == ROWS - 1:
+                nc.sync.dma_start(out=out[n * P:(n + 1) * P].rearrange("b o i j -> b (o i j)"), in_=stages[n][:])
+
+        load_x(0)
+        load_w(0)
+        load_x(1)
+        load_w(1)
+        load_w(2)
+        load_w(3)
+        load_x(2)
+        stage_x(0, 0)
+        stage_w(0)
+        stage_x(0, 1)
+        stage_w(1)
+        for n in range(NBT + 2):
+            if n + 3 < NBT:
+                load_x(n + 3)
+            for half in range(2):
+                m = n - 2 if half == 0 else n - 1
+                rows = (2, 3) if half == 0 else (0, 1)
+                if 0 <= n - 1 < NBT:
+                    quant_x(n - 1, 2 * half)
+                    quant_x(n - 1, 2 * half + 1)
+                if n < NBT:
+                    transpose_x(n, half)
+                    exit_x(n, half)
+                wrow = 2 * n + half
+                if wrow < ROWS:
+                    transpose_w(wrow)
+                    exit_w(wrow)
+                if 0 <= m < NBT:
+                    for i in rows:
+                        multiply(m, i)
+                    for i in rows:
+                        exit_out(m, i)
+                if n + 1 < NBT:
+                    stage_x(n + 1, half)
+                if wrow < ROWS:
+                    quant_w(wrow)
+                    if wrow + 2 < ROWS:
+                        stage_w(wrow + 2)

@@ -64,19 +64,19 @@ def tile_localconvolution_t_kernel(tc, x, weight, out):
                 for uh in range(2):
                     nc.vector.tensor_copy(out=wdst[:, uh], in_=wsrc[:, uh])
 
-        def transpose_w(i):
+        def transpose_w(i, js):
             wst32 = wsts[i][:].bitcast(F32)
-            for j in range(COLS):
+            for j in js:
                 pw = pt.tile([P, 4, P], F32, name="pw", tag="pt")
                 wbanks[(i, j)] = pw
                 for u in range(KH):
                     nc.tensor.transpose(pw[:, u, :], wst32[:, (j * 4 + u) * P:(j * 4 + u + 1) * P], ident[:])
 
-        def exit_w(i):
-            wg = wld.tile([P, COLS * 1024], BF16, name="wg", align_bytes=64)
-            wgs[i] = wg
-            wg32 = wg[:].bitcast(F32).rearrange("p (j q o r) -> p j q o r", j=COLS, q=2, o=O, r=2)
-            for j in range(COLS):
+        def exit_w(i, js):
+            if js[0] == 0:
+                wgs[i] = wld.tile([P, COLS * 1024], BF16, name="wg", align_bytes=64)
+            wg32 = wgs[i][:].bitcast(F32).rearrange("p (j q o r) -> p j q o r", j=COLS, q=2, o=O, r=2)
+            for j in js:
                 nc.scalar.copy(out=wg32[:, j], in_=wbanks[(i, j)][:].rearrange("p (r q) o -> p q o r", r=2, q=2))
 
         def quant_w(i):
@@ -85,26 +85,26 @@ def tile_localconvolution_t_kernel(tc, x, weight, out):
                 scales=ws[:, i * 1024:(i + 1) * 1024],
                 in_=wgs[i][:])
 
-        def stage_x(n, ch):
-            if ch == 0:
+        def stage_x(n, ch, hp):
+            if ch == 0 and hp == 0:
                 sts[n] = stg.tile([P, 8 * 2 * 3 * 128], BF16, name="st")
             st32 = sts[n][:].bitcast(F32)
             xw = (xts[n][0][:].bitcast(F32), xts[n][1][:].bitcast(F32))
             stv = st32.rearrange(
                 "p (s x c w g k e a) -> p x c g e s k a w", s=4, x=2, c=2, w=3, g=2, k=4, e=2, a=4)
-            for hp in range(2):
-                for e in range(2):
-                    nh = 4 - hp
-                    par = (e + hp + ch) % 2
-                    off = (49 * e + 7 * hp + ch - par) // 2
-                    src = xw[par][:, off:off + NW].rearrange(
-                        "p (g a k s r) -> p g s k a r", g=2, a=4, k=4, s=7, r=7)
-                    for gg in range(2):
-                        nc.vector.tensor_copy(out=stv[:, hp, ch, gg, e, 0:nh], in_=src[:, gg, 0:nh, :, :, 0:3])
+            for e in range(2):
+                nh = 4 - hp
+                par = (e + hp + ch) % 2
+                off = (49 * e + 7 * hp + ch - par) // 2
+                src = xw[par][:, off:off + NW].rearrange(
+                    "p (g a k s r) -> p g s k a r", g=2, a=4, k=4, s=7, r=7)
+                for gg in range(2):
+                    nc.vector.tensor_copy(out=stv[:, hp, ch, gg, e, 0:nh], in_=src[:, gg, 0:nh, :, :, 0:3])
 
-        def transpose_x(n, ch):
+        def transpose_x(n, j):
             st32 = sts[n][:].bitcast(F32)
-            for j in (ch, ch + 2):
+            ch = j % 2
+            if True:
                 for par in range(2):
                     pe = pt.tile([P, 4, P], F32, name="pe", tag="pt")
                     banks[(n, j, par)] = pe
@@ -112,11 +112,11 @@ def tile_localconvolution_t_kernel(tc, x, weight, out):
                         lo = ((h * 2 + ch) * 3 + j // 2) * 64
                         nc.tensor.transpose(pe[:, s, :], st32[:, lo:lo + P], ident[:])
 
-        def exit_x(n, ch):
-            if ch == 0:
+        def exit_x(n, j):
+            if j == 0:
                 gs[n] = grp.tile([P, NHB * COLS * P * 4], BF16, name="g", align_bytes=64)
             g32 = gs[n][:].bitcast(F32).rearrange("p (h j b r) -> p h j b r", h=NHB, j=COLS, b=P, r=2)
-            for j in (ch, ch + 2):
+            if True:
                 ev = banks[(n, j, 0)]
                 od = banks[(n, j, 1)]
                 nc.scalar.copy(out=g32[:, 0:5:4, j], in_=ev[:].rearrange("p (h r) b -> p h b r", h=2, r=2))
@@ -160,34 +160,34 @@ def tile_localconvolution_t_kernel(tc, x, weight, out):
         load_w(2)
         load_w(3)
         load_x(2)
-        stage_x(0, 0)
+        stage_x(0, 0, 0)
+        stage_x(0, 0, 1)
+        stage_x(0, 1, 0)
+        stage_x(0, 1, 1)
         stage_w(0)
-        stage_x(0, 1)
         stage_w(1)
+        JORDER = (0, 2, 1, 3)
         for n in range(NBT + 2):
             if n + 3 < NBT:
                 load_x(n + 3)
-            for half in range(2):
-                m = n - 2 if half == 0 else n - 1
-                rows = (2, 3) if half == 0 else (0, 1)
+            for k in range(4):
+                m, i = (n - 1, k - 1) if k > 0 else (n - 2, 3)
                 if 0 <= n - 1 < NBT:
-                    quant_x(n - 1, 2 * half)
-                    quant_x(n - 1, 2 * half + 1)
+                    quant_x(n - 1, k)
                 if n < NBT:
-                    transpose_x(n, half)
-                    exit_x(n, half)
-                wrow = 2 * n + half
+                    transpose_x(n, JORDER[k])
+                    exit_x(n, JORDER[k])
+                wrow = 2 * n + k // 2
                 if wrow < ROWS:
-                    transpose_w(wrow)
-                    exit_w(wrow)
+                    js = (0, 1) if k % 2 == 0 else (2, 3)
+                    transpose_w(wrow, js)
+                    exit_w(wrow, js)
                 if 0 <= m < NBT:
-                    for i in rows:
-                        multiply(m, i)
-                    for i in rows:
-                        exit_out(m, i)
+                    multiply(m, i)
+                    exit_out(m, i)
                 if n + 1 < NBT:
-                    stage_x(n + 1, half)
-                if wrow < ROWS:
+                    stage_x(n + 1, k // 2, k % 2)
+                if wrow < ROWS and k % 2 == 1:
                     quant_w(wrow)
                     if wrow + 2 < ROWS:
                         stage_w(wrow + 2)

@@ -27,8 +27,7 @@ def tile_localconvolution_t_kernel(tc, x, weight, out):
             tc.tile_pool(name="wl4", bufs=4) as wl4, \
             tc.tile_pool(name="wld", bufs=2) as wld, \
             tc.psum_pool(name="pt", bufs=4) as pt, \
-            tc.psum_pool(name="pa", bufs=4) as pa, \
-            tc.manual_schedule():
+            tc.psum_pool(name="pa", bufs=4) as pa:
         ident = const.tile([P, P], F32)
         make_identity(nc, ident[:])
         wc = const.tile([P, ROWS * COLS * 2 * O], U32, align_bytes=64)
@@ -64,19 +63,19 @@ def tile_localconvolution_t_kernel(tc, x, weight, out):
                 for uh in range(2):
                     nc.vector.tensor_copy(out=wdst[:, uh], in_=wsrc[:, uh])
 
-        def transpose_w(i, js):
+        def transpose_w(i):
             wst32 = wsts[i][:].bitcast(F32)
-            for j in js:
+            for j in range(COLS):
                 pw = pt.tile([P, 4, P], F32, name="pw", tag="pt")
                 wbanks[(i, j)] = pw
                 for u in range(KH):
                     nc.tensor.transpose(pw[:, u, :], wst32[:, (j * 4 + u) * P:(j * 4 + u + 1) * P], ident[:])
 
-        def exit_w(i, js):
-            if js[0] == 0:
-                wgs[i] = wld.tile([P, COLS * 1024], BF16, name="wg", align_bytes=64)
-            wg32 = wgs[i][:].bitcast(F32).rearrange("p (j q o r) -> p j q o r", j=COLS, q=2, o=O, r=2)
-            for j in js:
+        def exit_w(i):
+            wg = wld.tile([P, COLS * 1024], BF16, name="wg", align_bytes=64)
+            wgs[i] = wg
+            wg32 = wg[:].bitcast(F32).rearrange("p (j q o r) -> p j q o r", j=COLS, q=2, o=O, r=2)
+            for j in range(COLS):
                 nc.scalar.copy(out=wg32[:, j], in_=wbanks[(i, j)][:].rearrange("p (r q) o -> p q o r", r=2, q=2))
 
         def quant_w(i):
@@ -85,26 +84,26 @@ def tile_localconvolution_t_kernel(tc, x, weight, out):
                 scales=ws[:, i * 1024:(i + 1) * 1024],
                 in_=wgs[i][:])
 
-        def stage_x(n, ch, hp):
-            if ch == 0 and hp == 0:
+        def stage_x(n, ch):
+            if ch == 0:
                 sts[n] = stg.tile([P, 8 * 2 * 3 * 128], BF16, name="st")
             st32 = sts[n][:].bitcast(F32)
             xw = (xts[n][0][:].bitcast(F32), xts[n][1][:].bitcast(F32))
             stv = st32.rearrange(
                 "p (s x c w g k e a) -> p x c g e s k a w", s=4, x=2, c=2, w=3, g=2, k=4, e=2, a=4)
-            for e in range(2):
-                nh = 4 - hp
-                par = (e + hp + ch) % 2
-                off = (49 * e + 7 * hp + ch - par) // 2
-                src = xw[par][:, off:off + NW].rearrange(
-                    "p (g a k s r) -> p g s k a r", g=2, a=4, k=4, s=7, r=7)
-                for gg in range(2):
-                    nc.vector.tensor_copy(out=stv[:, hp, ch, gg, e, 0:nh], in_=src[:, gg, 0:nh, :, :, 0:3])
+            for hp in range(2):
+                for e in range(2):
+                    nh = 4 - hp
+                    par = (e + hp + ch) % 2
+                    off = (49 * e + 7 * hp + ch - par) // 2
+                    src = xw[par][:, off:off + NW].rearrange(
+                        "p (g a k s r) -> p g s k a r", g=2, a=4, k=4, s=7, r=7)
+                    for gg in range(2):
+                        nc.vector.tensor_copy(out=stv[:, hp, ch, gg, e, 0:nh], in_=src[:, gg, 0:nh, :, :, 0:3])
 
-        def transpose_x(n, j):
+        def transpose_x(n, ch):
             st32 = sts[n][:].bitcast(F32)
-            ch = j % 2
-            if True:
+            for j in (ch, ch + 2):
                 for par in range(2):
                     pe = pt.tile([P, 4, P], F32, name="pe", tag="pt")
                     banks[(n, j, par)] = pe
@@ -112,11 +111,11 @@ def tile_localconvolution_t_kernel(tc, x, weight, out):
                         lo = ((h * 2 + ch) * 3 + j // 2) * 64
                         nc.tensor.transpose(pe[:, s, :], st32[:, lo:lo + P], ident[:])
 
-        def exit_x(n, j):
-            if j == 0:
+        def exit_x(n, ch):
+            if ch == 0:
                 gs[n] = grp.tile([P, NHB * COLS * P * 4], BF16, name="g", align_bytes=64)
             g32 = gs[n][:].bitcast(F32).rearrange("p (h j b r) -> p h j b r", h=NHB, j=COLS, b=P, r=2)
-            if True:
+            for j in (ch, ch + 2):
                 ev = banks[(n, j, 0)]
                 od = banks[(n, j, 1)]
                 nc.scalar.copy(out=g32[:, 0:5:4, j], in_=ev[:].rearrange("p (h r) b -> p h b r", h=2, r=2))
@@ -160,34 +159,34 @@ def tile_localconvolution_t_kernel(tc, x, weight, out):
         load_w(2)
         load_w(3)
         load_x(2)
-        stage_x(0, 0, 0)
-        stage_x(0, 0, 1)
-        stage_x(0, 1, 0)
-        stage_x(0, 1, 1)
+        stage_x(0, 0)
         stage_w(0)
+        stage_x(0, 1)
         stage_w(1)
-        JORDER = (0, 2, 1, 3)
         for n in range(NBT + 2):
             if n + 3 < NBT:
                 load_x(n + 3)
-            for k in range(4):
-                m, i = (n - 1, k - 1) if k > 0 else (n - 2, 3)
+            for half in range(2):
+                m = n - 2 if half == 0 else n - 1
+                rows = (2, 3) if half == 0 else (0, 1)
                 if 0 <= n - 1 < NBT:
-                    quant_x(n - 1, k)
+                    quant_x(n - 1, 2 * half)
+                    quant_x(n - 1, 2 * half + 1)
                 if n < NBT:
-                    transpose_x(n, JORDER[k])
-                    exit_x(n, JORDER[k])
-                wrow = 2 * n + k // 2
+                    transpose_x(n, half)
+                    exit_x(n, half)
+                wrow = 2 * n + half
                 if wrow < ROWS:
-                    js = (0, 1) if k % 2 == 0 else (2, 3)
-                    transpose_w(wrow, js)
-                    exit_w(wrow, js)
+                    transpose_w(wrow)
+                    exit_w(wrow)
                 if 0 <= m < NBT:
-                    multiply(m, i)
-                    exit_out(m, i)
+                    for i in rows:
+                        multiply(m, i)
+                    for i in rows:
+                        exit_out(m, i)
                 if n + 1 < NBT:
-                    stage_x(n + 1, k // 2, k % 2)
-                if wrow < ROWS and k % 2 == 1:
+                    stage_x(n + 1, half)
+                if wrow < ROWS:
                     quant_w(wrow)
                     if wrow + 2 < ROWS:
                         stage_w(wrow + 2)

@@ -22,9 +22,9 @@ def tile_localconvolution_t_kernel(tc, x, weight, out):
             tc.tile_pool(name="xin", bufs=3) as xin, \
             tc.tile_pool(name="stg", bufs=2) as stg, \
             tc.tile_pool(name="grp", bufs=2) as grp, \
-            tc.tile_pool(name="cod", bufs=4) as cod, \
+            tc.tile_pool(name="cod", bufs=6) as cod, \
             tc.tile_pool(name="res", bufs=2) as res, \
-            tc.tile_pool(name="wl4", bufs=4) as wl4, \
+            tc.tile_pool(name="wl4", bufs=3) as wl4, \
             tc.tile_pool(name="wld", bufs=2) as wld, \
             tc.psum_pool(name="pt", bufs=4) as pt, \
             tc.psum_pool(name="pa", bufs=4) as pa:
@@ -144,11 +144,39 @@ def tile_localconvolution_t_kernel(tc, x, weight, out):
                         rhs=wc[:, wo:wo + O].bitcast(FP8X4), rhs_scale=ws[:, wo:wo + O],
                         start=(q == 0), stop=(q == 1))
 
+        def quant_last(n, j):
+            for i in range(ROWS):
+                if j == 0:
+                    pc = cod.tile([P, 1024], U32, name="pc", align_bytes=64)
+                    psc = cod.tile([P, 1024], U8, name="psc", align_bytes=64)
+                    codes[(n, i)] = (pc, psc)
+                pc, psc = codes[(n, i)]
+                for q in range(2):
+                    lo = q * 512 + j * P
+                    src = ((i + q) * COLS + j) * 512
+                    nc.vector.quantize_mx(out=pc[:, lo:lo + P].bitcast(FP8X4), scales=psc[:, lo:lo + P],
+                                          in_=gs[n][:, src:src + 512])
+
+        def multiply_last(n, j):
+            for i in range(ROWS):
+                if j == 0:
+                    accs[(n, i)] = pa.tile([P, COLS * O], F32, name="acc")
+                pc, psc = codes[(n, i)]
+                for q in range(2):
+                    lo = q * 512 + j * P
+                    wo = ((i * COLS + j) * 2 + q) * O
+                    nc.tensor.matmul_mx(
+                        out=accs[(n, i)][:, j * O:(j + 1) * O],
+                        lhsT=pc[:, lo:lo + P].bitcast(FP8X4), lhsT_scale=psc[:, lo:lo + P],
+                        rhs=wc[:, wo:wo + O].bitcast(FP8X4), rhs_scale=ws[:, wo:wo + O],
+                        start=(q == 0), stop=(q == 1))
+
         def exit_out(n, i):
             if i == 0:
                 stages[n] = res.tile([P, O * ROWS * COLS], F32, name="stage")
             sgv = stages[n][:].rearrange("p (o i j) -> p o i j", o=O, i=ROWS, j=COLS)
-            nc.scalar.copy(out=sgv[:, :, i, :], in_=accs[(n, i)][:].rearrange("p (j o) -> p o j", j=COLS))
+            eng = nc.vector.tensor_copy if n == NBT - 1 and i >= 2 else nc.scalar.copy
+            eng(out=sgv[:, :, i, :], in_=accs[(n, i)][:].rearrange("p (j o) -> p o j", j=COLS))
             if i == ROWS - 1:
                 nc.sync.dma_start(out=out[n * P:(n + 1) * P].rearrange("b o i j -> b (o i j)"), in_=stages[n][:])
 
@@ -163,7 +191,7 @@ def tile_localconvolution_t_kernel(tc, x, weight, out):
         stage_w(0)
         stage_x(0, 1)
         stage_w(1)
-        for n in range(NBT + 2):
+        for n in range(NBT):
             if n + 3 < NBT:
                 load_x(n + 3)
             for half in range(2):
@@ -190,3 +218,13 @@ def tile_localconvolution_t_kernel(tc, x, weight, out):
                     quant_w(wrow)
                     if wrow + 2 < ROWS:
                         stage_w(wrow + 2)
+        last = NBT - 1
+        for i in (2, 3):
+            multiply(last - 1, i)
+        for i in (2, 3):
+            exit_out(last - 1, i)
+        for j in (0, 2, 1, 3):
+            quant_last(last, j)
+            multiply_last(last, j)
+        for i in (0, 2, 1, 3):
+            exit_out(last, i)

@@ -12,6 +12,7 @@ B, C, O, ROWS, COLS, KH, KW, H, W = 1024, 64, 128, 4, 4, 4, 4, 7, 7
 FLOPS = 2 * ROWS * COLS * B * O * C * KH * KW
 NBT = B // P
 NHB = 5
+GW = NHB * COLS * P * 4
 XPAD = 3200
 NW = C * H * W // 2
 
@@ -38,9 +39,12 @@ def tile_localconvolution_t_kernel(tc, x, weight, out):
         def load_x(n):
             rows = x[n * P:(n + 1) * P].rearrange("b c h w -> b (c h w)")
             x0 = xin.tile([P, XPAD], BF16, name="x0")
-            nc.sync.dma_start(out=x0[:, 0:C * H * W], in_=rows)
             x1 = xin.tile([P, XPAD], BF16, name="x1")
-            nc.sync.dma_start(out=x1[:, 0:C * H * W - 1], in_=rows[:, 1:C * H * W])
+            cuts = (0, NW, 2 * NW) if n == 0 else (0, 2 * NW)
+            for lo, hi in zip(cuts[:-1], cuts[1:]):
+                nc.sync.dma_start(out=x0[:, lo:hi], in_=rows[:, lo:hi])
+                top = min(hi, 2 * NW - 1)
+                nc.sync.dma_start(out=x1[:, lo:top], in_=rows[:, lo + 1:top + 1])
             xts[n] = (x0, x1)
 
         def load_w(i):
@@ -91,15 +95,14 @@ def tile_localconvolution_t_kernel(tc, x, weight, out):
             xw = (xts[n][0][:].bitcast(F32), xts[n][1][:].bitcast(F32))
             stv = st32.rearrange(
                 "p (s x c w g k e a) -> p x c g e s k a w", s=4, x=2, c=2, w=3, g=2, k=4, e=2, a=4)
-            for hp in range(2):
+            for gg, hp in ((0, 0), (0, 1), (1, 0), (1, 1)):
                 for e in range(2):
                     nh = 4 - hp
                     par = (e + hp + ch) % 2
                     off = (49 * e + 7 * hp + ch - par) // 2
                     src = xw[par][:, off:off + NW].rearrange(
                         "p (g a k s r) -> p g s k a r", g=2, a=4, k=4, s=7, r=7)
-                    for gg in range(2):
-                        nc.vector.tensor_copy(out=stv[:, hp, ch, gg, e, 0:nh], in_=src[:, gg, 0:nh, :, :, 0:3])
+                    nc.vector.tensor_copy(out=stv[:, hp, ch, gg, e, 0:nh], in_=src[:, gg, 0:nh, :, :, 0:3])
 
         def transpose_x(n, ch):
             st32 = sts[n][:].bitcast(F32)
@@ -113,16 +116,26 @@ def tile_localconvolution_t_kernel(tc, x, weight, out):
 
         def exit_x(n, ch):
             if ch == 0:
-                gs[n] = grp.tile([P, NHB * COLS * P * 4], BF16, name="g", align_bytes=64)
-            g32 = gs[n][:].bitcast(F32).rearrange("p (h j b r) -> p h j b r", h=NHB, j=COLS, b=P, r=2)
+                gs[n] = grp.tile([P, GW + 64], BF16, name="g", align_bytes=64)
+            flat = gs[n][:].bitcast(F32)
+            g32 = flat[:, 0:GW // 2].rearrange("p (h j b r) -> p h j b r", h=NHB, j=COLS, b=P, r=2)
             for j in (ch, ch + 2):
                 ev = banks[(n, j, 0)]
                 od = banks[(n, j, 1)]
                 nc.scalar.copy(out=g32[:, 0:5:4, j], in_=ev[:].rearrange("p (h r) b -> p h b r", h=2, r=2))
-                nc.scalar.copy(out=g32[:, 2, j], in_=ev[:, 1:3, :].rearrange("p r b -> p b r"))
+                if j < 1:
+                    nc.scalar.copy(out=g32[:, 2, j], in_=ev[:, 1:3, :].rearrange("p r b -> p b r"))
                 nc.scalar.copy(out=g32[:, 1, j], in_=od[:, 0:2, :].rearrange("p r b -> p b r"))
-                eng = nc.vector.tensor_copy if j >= 2 else nc.scalar.copy
-                eng(out=g32[:, 3, j], in_=od[:, 1:3, :].rearrange("p r b -> p b r"))
+                nc.scalar.copy(out=g32[:, 3, j], in_=od[:, 1:3, :].rearrange("p r b -> p b r"))
+
+        def pair_x(n, ch):
+            flat = gs[n][:].bitcast(F32)
+            g32 = flat[:, 0:GW // 2].rearrange("p (h j b r) -> p h j b r", h=NHB, j=COLS, b=P, r=2)
+            for j in (ch, ch + 2):
+                if j >= 1:
+                    lo = j * 2 * P + 1
+                    pair = flat[:, lo:lo + 4368].rearrange("p (x y) -> p y x", y=273)[:, 0:2 * P:2, 0:16:15]
+                    nc.vector.tensor_copy(out=g32[:, 2, j], in_=pair)
 
         def quant_x(n, i):
             pc = cod.tile([P, 1024], U32, name="pc", align_bytes=64)
@@ -175,21 +188,32 @@ def tile_localconvolution_t_kernel(tc, x, weight, out):
             if i == 0:
                 stages[n] = res.tile([P, O * ROWS * COLS], F32, name="stage")
             sgv = stages[n][:].rearrange("p (o i j) -> p o i j", o=O, i=ROWS, j=COLS)
-            eng = nc.vector.tensor_copy if n == NBT - 1 and i >= 2 else nc.scalar.copy
-            eng(out=sgv[:, :, i, :], in_=accs[(n, i)][:].rearrange("p (j o) -> p o j", j=COLS))
+            nc.scalar.copy(out=sgv[:, :, i, :], in_=accs[(n, i)][:].rearrange("p (j o) -> p o j", j=COLS))
             if i == ROWS - 1:
                 nc.sync.dma_start(out=out[n * P:(n + 1) * P].rearrange("b o i j -> b (o i j)"), in_=stages[n][:])
 
+        def exit_last(n):
+            stage = res.tile([P, O * ROWS * COLS], F32, name="stage")
+            sgv = stage[:].rearrange("p (o i j) -> p o i j", o=O, i=ROWS, j=COLS)
+            rows = out[n * P:(n + 1) * P].rearrange("b o i j -> b (o i j)")
+            for half in range(2):
+                span = slice(half * O // 2, (half + 1) * O // 2)
+                for i in (0, 2, 1, 3):
+                    eng = nc.vector.tensor_copy if i >= 2 else nc.scalar.copy
+                    eng(out=sgv[:, span, i, :], in_=accs[(n, i)][:].rearrange("p (j o) -> p o j", j=COLS)[:, span])
+                lo, hi = span.start * ROWS * COLS, span.stop * ROWS * COLS
+                nc.sync.dma_start(out=rows[:, lo:hi], in_=stage[:, lo:hi])
+
         load_x(0)
         load_w(0)
-        load_x(1)
         load_w(1)
+        load_x(1)
         load_w(2)
         load_w(3)
         load_x(2)
         stage_x(0, 0)
-        stage_w(0)
         stage_x(0, 1)
+        stage_w(0)
         stage_w(1)
         for n in range(NBT):
             if n + 3 < NBT:
@@ -214,6 +238,8 @@ def tile_localconvolution_t_kernel(tc, x, weight, out):
                         exit_out(m, i)
                 if n + 1 < NBT:
                     stage_x(n + 1, half)
+                if n < NBT:
+                    pair_x(n, half)
                 if wrow < ROWS:
                     quant_w(wrow)
                     if wrow + 2 < ROWS:
@@ -226,5 +252,4 @@ def tile_localconvolution_t_kernel(tc, x, weight, out):
         for j in (0, 2, 1, 3):
             quant_last(last, j)
             multiply_last(last, j)
-        for i in (0, 2, 1, 3):
-            exit_out(last, i)
+        exit_last(last)

@@ -36,15 +36,20 @@ def tile_localconvolution_t_kernel(tc, x, weight, out):
         xts, sts, gs, banks, codes, accs, stages = {}, {}, {}, {}, {}, {}, {}
         wraws, wsts, wgs, wbanks = {}, {}, {}, {}
 
+        def col(j):
+            return (j % 2) * 2 + j // 2
+
         def load_x(n):
             rows = x[n * P:(n + 1) * P].rearrange("b c h w -> b (c h w)")
             x0 = xin.tile([P, XPAD], BF16, name="x0")
             x1 = xin.tile([P, XPAD], BF16, name="x1")
-            cuts = (0, NW, 2 * NW) if n == 0 else (0, 2 * NW)
-            for lo, hi in zip(cuts[:-1], cuts[1:]):
-                nc.sync.dma_start(out=x0[:, lo:hi], in_=rows[:, lo:hi])
-                top = min(hi, 2 * NW - 1)
-                nc.sync.dma_start(out=x1[:, lo:top], in_=rows[:, lo + 1:top + 1])
+            if n == 0:
+                for lo, hi in ((0, NW), (NW, 2 * NW)):
+                    nc.sync.dma_start(out=x0[:, lo:hi], in_=rows[:, lo:hi])
+                nc.scalar.copy(out=x1[:, 0:NW - 1], in_=x0[:, 1:NW])
+            else:
+                nc.sync.dma_start(out=x0[:, 0:2 * NW], in_=rows)
+                nc.sync.dma_start(out=x1[:, 0:2 * NW - 1], in_=rows[:, 1:2 * NW])
             xts[n] = (x0, x1)
 
         def load_w(i):
@@ -80,7 +85,8 @@ def tile_localconvolution_t_kernel(tc, x, weight, out):
             wgs[i] = wg
             wg32 = wg[:].bitcast(F32).rearrange("p (j q o r) -> p j q o r", j=COLS, q=2, o=O, r=2)
             for j in range(COLS):
-                nc.scalar.copy(out=wg32[:, j], in_=wbanks[(i, j)][:].rearrange("p (r q) o -> p q o r", r=2, q=2))
+                eng = nc.vector.tensor_copy if i == 0 and j >= 2 else nc.scalar.copy
+                eng(out=wg32[:, j], in_=wbanks[(i, j)][:].rearrange("p (r q) o -> p q o r", r=2, q=2))
 
         def quant_w(i):
             nc.vector.quantize_mx(
@@ -88,17 +94,17 @@ def tile_localconvolution_t_kernel(tc, x, weight, out):
                 scales=ws[:, i * 1024:(i + 1) * 1024],
                 in_=wgs[i][:])
 
-        def stage_x(n, ch):
-            if ch == 0:
+        def stage_x(n, ch, parts):
+            if n not in sts:
                 sts[n] = stg.tile([P, 8 * 2 * 3 * 128], BF16, name="st")
             st32 = sts[n][:].bitcast(F32)
             xw = (xts[n][0][:].bitcast(F32), xts[n][1][:].bitcast(F32))
             stv = st32.rearrange(
                 "p (s x c w g k e a) -> p x c g e s k a w", s=4, x=2, c=2, w=3, g=2, k=4, e=2, a=4)
-            for gg, hp in ((0, 0), (0, 1), (1, 0), (1, 1)):
-                for e in range(2):
+            for gg, par in parts:
+                for hp in range(2):
                     nh = 4 - hp
-                    par = (e + hp + ch) % 2
+                    e = (par + hp + ch) % 2
                     off = (49 * e + 7 * hp + ch - par) // 2
                     src = xw[par][:, off:off + NW].rearrange(
                         "p (g a k s r) -> p g s k a r", g=2, a=4, k=4, s=7, r=7)
@@ -116,26 +122,25 @@ def tile_localconvolution_t_kernel(tc, x, weight, out):
 
         def exit_x(n, ch):
             if ch == 0:
-                gs[n] = grp.tile([P, GW + 64], BF16, name="g", align_bytes=64)
+                gs[n] = grp.tile([P, GW + 640], BF16, name="g", align_bytes=64)
             flat = gs[n][:].bitcast(F32)
             g32 = flat[:, 0:GW // 2].rearrange("p (h j b r) -> p h j b r", h=NHB, j=COLS, b=P, r=2)
             for j in (ch, ch + 2):
+                jp = col(j)
                 ev = banks[(n, j, 0)]
                 od = banks[(n, j, 1)]
-                nc.scalar.copy(out=g32[:, 0:5:4, j], in_=ev[:].rearrange("p (h r) b -> p h b r", h=2, r=2))
-                if j < 1:
-                    nc.scalar.copy(out=g32[:, 2, j], in_=ev[:, 1:3, :].rearrange("p r b -> p b r"))
-                nc.scalar.copy(out=g32[:, 1, j], in_=od[:, 0:2, :].rearrange("p r b -> p b r"))
-                nc.scalar.copy(out=g32[:, 3, j], in_=od[:, 1:3, :].rearrange("p r b -> p b r"))
+                nc.scalar.copy(out=g32[:, 0:5:4, jp], in_=ev[:].rearrange("p (h r) b -> p h b r", h=2, r=2))
+                if jp < 2 or n >= NBT - 2:
+                    nc.scalar.copy(out=g32[:, 2, jp], in_=ev[:, 1:3, :].rearrange("p r b -> p b r"))
+                nc.scalar.copy(out=g32[:, 1, jp], in_=od[:, 0:2, :].rearrange("p r b -> p b r"))
+                nc.scalar.copy(out=g32[:, 3, jp], in_=od[:, 1:3, :].rearrange("p r b -> p b r"))
 
-        def pair_x(n, ch):
+        def pair_x(n):
             flat = gs[n][:].bitcast(F32)
             g32 = flat[:, 0:GW // 2].rearrange("p (h j b r) -> p h j b r", h=NHB, j=COLS, b=P, r=2)
-            for j in (ch, ch + 2):
-                if j >= 1:
-                    lo = j * 2 * P + 1
-                    pair = flat[:, lo:lo + 4368].rearrange("p (x y) -> p y x", y=273)[:, 0:2 * P:2, 0:16:15]
-                    nc.vector.tensor_copy(out=g32[:, 2, j], in_=pair)
+            lo = 2 * 2 * P + 1
+            pair = flat[:, lo:lo + 6 * 819].rearrange("p (x y) -> p y x", y=819)[:, 0:4 * P:2, 0:6:5]
+            nc.vector.tensor_copy(out=g32[:, 2, 2:4], in_=pair.rearrange("p (j b) r -> p j b r", b=P))
 
         def quant_x(n, i):
             pc = cod.tile([P, 1024], U32, name="pc", align_bytes=64)
@@ -143,13 +148,14 @@ def tile_localconvolution_t_kernel(tc, x, weight, out):
             codes[(n, i)] = (pc, psc)
             nc.vector.quantize_mx(out=pc[:].bitcast(FP8X4), scales=psc[:], in_=gs[n][:, i * 2048:i * 2048 + 4096])
 
-        def multiply(n, i):
+        def multiply(n, i, js=(0, 1, 2, 3)):
             pc, psc = codes[(n, i)]
-            acc = pa.tile([P, COLS * O], F32, name="acc")
-            accs[(n, i)] = acc
-            for j in range(COLS):
+            if js[0] == 0:
+                accs[(n, i)] = pa.tile([P, COLS * O], F32, name="acc")
+            acc = accs[(n, i)]
+            for j in js:
                 for q in range(2):
-                    lo = q * 512 + j * P
+                    lo = q * 512 + col(j) * P
                     wo = ((i * COLS + j) * 2 + q) * O
                     nc.tensor.matmul_mx(
                         out=acc[:, j * O:(j + 1) * O],
@@ -157,32 +163,17 @@ def tile_localconvolution_t_kernel(tc, x, weight, out):
                         rhs=wc[:, wo:wo + O].bitcast(FP8X4), rhs_scale=ws[:, wo:wo + O],
                         start=(q == 0), stop=(q == 1))
 
-        def quant_last(n, j):
-            for i in range(ROWS):
-                if j == 0:
-                    pc = cod.tile([P, 1024], U32, name="pc", align_bytes=64)
-                    psc = cod.tile([P, 1024], U8, name="psc", align_bytes=64)
-                    codes[(n, i)] = (pc, psc)
-                pc, psc = codes[(n, i)]
-                for q in range(2):
-                    lo = q * 512 + j * P
-                    src = ((i + q) * COLS + j) * 512
-                    nc.vector.quantize_mx(out=pc[:, lo:lo + P].bitcast(FP8X4), scales=psc[:, lo:lo + P],
-                                          in_=gs[n][:, src:src + 512])
-
-        def multiply_last(n, j):
-            for i in range(ROWS):
-                if j == 0:
-                    accs[(n, i)] = pa.tile([P, COLS * O], F32, name="acc")
-                pc, psc = codes[(n, i)]
-                for q in range(2):
-                    lo = q * 512 + j * P
-                    wo = ((i * COLS + j) * 2 + q) * O
-                    nc.tensor.matmul_mx(
-                        out=accs[(n, i)][:, j * O:(j + 1) * O],
-                        lhsT=pc[:, lo:lo + P].bitcast(FP8X4), lhsT_scale=psc[:, lo:lo + P],
-                        rhs=wc[:, wo:wo + O].bitcast(FP8X4), rhs_scale=ws[:, wo:wo + O],
-                        start=(q == 0), stop=(q == 1))
+        def quant_last(n, i, half):
+            if half == 0:
+                pc = cod.tile([P, 1024], U32, name="pc", align_bytes=64)
+                psc = cod.tile([P, 1024], U8, name="psc", align_bytes=64)
+                codes[(n, i)] = (pc, psc)
+            pc, psc = codes[(n, i)]
+            for q in range(2):
+                lo = q * 512 + half * 2 * P
+                src = ((i + q) * COLS + half * 2) * 512
+                nc.vector.quantize_mx(out=pc[:, lo:lo + 2 * P].bitcast(FP8X4), scales=psc[:, lo:lo + 2 * P],
+                                      in_=gs[n][:, src:src + 1024])
 
         def exit_out(n, i):
             if i == 0:
@@ -192,17 +183,16 @@ def tile_localconvolution_t_kernel(tc, x, weight, out):
             if i == ROWS - 1:
                 nc.sync.dma_start(out=out[n * P:(n + 1) * P].rearrange("b o i j -> b (o i j)"), in_=stages[n][:])
 
-        def exit_last(n):
-            stage = res.tile([P, O * ROWS * COLS], F32, name="stage")
-            sgv = stage[:].rearrange("p (o i j) -> p o i j", o=O, i=ROWS, j=COLS)
+        def exit_last(n, i, span, eng):
+            if i == 0:
+                stages[n] = res.tile([P, O * ROWS * COLS], F32, name="stage")
+            sgv = stages[n][:].rearrange("p (o i j) -> p o i j", o=O, i=ROWS, j=COLS)
+            eng(out=sgv[:, span, i, :], in_=accs[(n, i)][:].rearrange("p (j o) -> p o j", j=COLS)[:, span])
+
+        def store_last(n, half):
             rows = out[n * P:(n + 1) * P].rearrange("b o i j -> b (o i j)")
-            for half in range(2):
-                span = slice(half * O // 2, (half + 1) * O // 2)
-                for i in (0, 2, 1, 3):
-                    eng = nc.vector.tensor_copy if i >= 2 else nc.scalar.copy
-                    eng(out=sgv[:, span, i, :], in_=accs[(n, i)][:].rearrange("p (j o) -> p o j", j=COLS)[:, span])
-                lo, hi = span.start * ROWS * COLS, span.stop * ROWS * COLS
-                nc.sync.dma_start(out=rows[:, lo:hi], in_=stage[:, lo:hi])
+            lo, hi = half * 1024, (half + 1) * 1024
+            nc.sync.dma_start(out=rows[:, lo:hi], in_=stages[n][:, lo:hi])
 
         load_x(0)
         load_w(0)
@@ -211,10 +201,15 @@ def tile_localconvolution_t_kernel(tc, x, weight, out):
         load_w(2)
         load_w(3)
         load_x(2)
-        stage_x(0, 0)
-        stage_x(0, 1)
-        stage_w(0)
-        stage_w(1)
+        with tc.manual_schedule(engines={mybir.EngineType.DVE}):
+            stage_x(0, 0, ((0, 0),))
+            stage_x(0, 1, ((0, 0),))
+            x0, x1 = xts[0]
+            nc.vector.tensor_copy(out=x1[:, NW:2 * NW - 1], in_=x0[:, NW + 1:2 * NW])
+            stage_x(0, 0, ((1, 0), (0, 1), (1, 1)))
+            stage_x(0, 1, ((1, 0), (0, 1), (1, 1)))
+            stage_w(0)
+            stage_w(1)
         for n in range(NBT):
             if n + 3 < NBT:
                 load_x(n + 3)
@@ -237,9 +232,9 @@ def tile_localconvolution_t_kernel(tc, x, weight, out):
                     for i in rows:
                         exit_out(m, i)
                 if n + 1 < NBT:
-                    stage_x(n + 1, half)
-                if n < NBT:
-                    pair_x(n, half)
+                    stage_x(n + 1, half, ((0, 0), (0, 1), (1, 0), (1, 1)))
+                if half == 1 and n < NBT - 2:
+                    pair_x(n)
                 if wrow < ROWS:
                     quant_w(wrow)
                     if wrow + 2 < ROWS:
@@ -249,7 +244,12 @@ def tile_localconvolution_t_kernel(tc, x, weight, out):
             multiply(last - 1, i)
         for i in (2, 3):
             exit_out(last - 1, i)
-        for j in (0, 2, 1, 3):
-            quant_last(last, j)
-            multiply_last(last, j)
-        exit_last(last)
+        for half in range(2):
+            for i in range(ROWS):
+                quant_last(last, i, half)
+                multiply(last, i, (half, half + 2))
+        for i in range(ROWS - 1):
+            exit_last(last, i, slice(0, O), nc.scalar.copy)
+        for half in range(2):
+            exit_last(last, ROWS - 1, slice(half * O // 2, (half + 1) * O // 2), nc.vector.tensor_copy)
+            store_last(last, half)

@@ -14,6 +14,7 @@ NBT = B // P
 NHB = 5
 GW = NHB * COLS * P * 4
 XPAD = 3200
+QUARTER = C * H * W // 4
 NW = C * H * W // 2
 
 
@@ -43,14 +44,20 @@ def tile_localconvolution_t_kernel(tc, x, weight, out):
             rows = x[n * P:(n + 1) * P].rearrange("b c h w -> b (c h w)")
             x0 = xin.tile([P, XPAD], BF16, name="x0")
             x1 = xin.tile([P, XPAD], BF16, name="x1")
+            xts[n] = (x0, x1)
             if n == 0:
-                for lo, hi in ((0, NW), (NW, 2 * NW)):
-                    nc.sync.dma_start(out=x0[:, lo:hi], in_=rows[:, lo:hi])
-                nc.scalar.copy(out=x1[:, 0:NW - 1], in_=x0[:, 1:NW])
+                for lo in range(0, 2 * NW, QUARTER):
+                    nc.sync.dma_start(out=x0[:, lo:lo + QUARTER], in_=rows[:, lo:lo + QUARTER])
+                for part in (0, 2):
+                    shift_part(nc.scalar.copy, part)
             else:
                 nc.sync.dma_start(out=x0[:, 0:2 * NW], in_=rows)
                 nc.sync.dma_start(out=x1[:, 0:2 * NW - 1], in_=rows[:, 1:2 * NW])
-            xts[n] = (x0, x1)
+
+        def shift_part(copy, part):
+            x0, x1 = xts[0]
+            lo, hi = part * QUARTER, (part + 1) * QUARTER
+            copy(out=x1[:, lo:hi - 1], in_=x0[:, lo + 1:hi])
 
         def load_w(i):
             wraw = wl4.tile([P, COLS * 1024], BF16, name="wraw")
@@ -130,7 +137,7 @@ def tile_localconvolution_t_kernel(tc, x, weight, out):
                 ev = banks[(n, j, 0)]
                 od = banks[(n, j, 1)]
                 nc.scalar.copy(out=g32[:, 0:5:4, jp], in_=ev[:].rearrange("p (h r) b -> p h b r", h=2, r=2))
-                if jp < 2 or n >= NBT - 2:
+                if jp < 2:
                     nc.scalar.copy(out=g32[:, 2, jp], in_=ev[:, 1:3, :].rearrange("p r b -> p b r"))
                 nc.scalar.copy(out=g32[:, 1, jp], in_=od[:, 0:2, :].rearrange("p r b -> p b r"))
                 nc.scalar.copy(out=g32[:, 3, jp], in_=od[:, 1:3, :].rearrange("p r b -> p b r"))
@@ -202,12 +209,11 @@ def tile_localconvolution_t_kernel(tc, x, weight, out):
         load_w(3)
         load_x(2)
         with tc.manual_schedule(engines={mybir.EngineType.DVE}):
-            stage_x(0, 0, ((0, 0),))
-            stage_x(0, 1, ((0, 0),))
-            x0, x1 = xts[0]
-            nc.vector.tensor_copy(out=x1[:, NW:2 * NW - 1], in_=x0[:, NW + 1:2 * NW])
-            stage_x(0, 0, ((1, 0), (0, 1), (1, 1)))
-            stage_x(0, 1, ((1, 0), (0, 1), (1, 1)))
+            shift_part(nc.vector.tensor_copy, 1)
+            stage_x(0, 0, ((0, 0), (0, 1)))
+            shift_part(nc.vector.tensor_copy, 3)
+            stage_x(0, 0, ((1, 0), (1, 1)))
+            stage_x(0, 1, ((0, 0), (0, 1), (1, 0), (1, 1)))
             stage_w(0)
             stage_w(1)
         for n in range(NBT):
@@ -231,23 +237,27 @@ def tile_localconvolution_t_kernel(tc, x, weight, out):
                         multiply(m, i)
                     for i in rows:
                         exit_out(m, i)
-                if n + 1 < NBT:
-                    stage_x(n + 1, half, ((0, 0), (0, 1), (1, 0), (1, 1)))
-                if half == 1 and n < NBT - 2:
-                    pair_x(n)
                 if wrow < ROWS:
                     quant_w(wrow)
-                    if wrow + 2 < ROWS:
-                        stage_w(wrow + 2)
+                if n + 1 < NBT:
+                    stage_x(n + 1, half, ((0, 0), (0, 1), (1, 0), (1, 1)))
+                if half == 1:
+                    pair_x(n)
+                if wrow + 2 < ROWS:
+                    stage_w(wrow + 2)
         last = NBT - 1
         for i in (2, 3):
             multiply(last - 1, i)
         for i in (2, 3):
             exit_out(last - 1, i)
-        for half in range(2):
-            for i in range(ROWS):
-                quant_last(last, i, half)
-                multiply(last, i, (half, half + 2))
+        for i in range(ROWS):
+            if i in (0, 3):
+                for half in range(2):
+                    quant_last(last, i, half)
+                    multiply(last, i, (half, half + 2))
+            else:
+                quant_x(last, i)
+                multiply(last, i)
         for i in range(ROWS - 1):
             exit_last(last, i, slice(0, O), nc.scalar.copy)
         for half in range(2):

@@ -57,13 +57,15 @@ def tile_localconvolution_t_kernel(tc, x, weight, out):
         def shift_part(copy, part):
             x0, x1 = xts[0]
             lo, hi = part * QUARTER, (part + 1) * QUARTER
-            copy(out=x1[:, lo:hi - 1], in_=x0[:, lo + 1:hi])
+            copy(out=x1[:, lo:hi - 2], in_=x0[:, lo + 1:hi - 1])
 
         def load_w(i):
             wraw = wl4.tile([P, COLS * 1024], BF16, name="wraw")
-            nc.sync.dma_start(
-                out=wraw[:].rearrange("o (j k) -> o j k", j=COLS),
-                in_=weight[i].rearrange("j o c u v -> o j (c u v)"))
+            step = 2 if i < 2 else COLS
+            for j in range(0, COLS, step):
+                nc.sync.dma_start(
+                    out=wraw[:].rearrange("o (j k) -> o j k", j=COLS)[:, j:j + step],
+                    in_=weight[i].rearrange("j o c u v -> o j (c u v)")[:, j:j + step])
             wraws[i] = wraw
 
         def stage_w(i):
@@ -92,8 +94,7 @@ def tile_localconvolution_t_kernel(tc, x, weight, out):
             wgs[i] = wg
             wg32 = wg[:].bitcast(F32).rearrange("p (j q o r) -> p j q o r", j=COLS, q=2, o=O, r=2)
             for j in range(COLS):
-                eng = nc.vector.tensor_copy if i == 0 and j >= 2 else nc.scalar.copy
-                eng(out=wg32[:, j], in_=wbanks[(i, j)][:].rearrange("p (r q) o -> p q o r", r=2, q=2))
+                nc.scalar.copy(out=wg32[:, j], in_=wbanks[(i, j)][:].rearrange("p (r q) o -> p q o r", r=2, q=2))
 
         def quant_w(i):
             nc.vector.quantize_mx(
@@ -107,15 +108,15 @@ def tile_localconvolution_t_kernel(tc, x, weight, out):
             st32 = sts[n][:].bitcast(F32)
             xw = (xts[n][0][:].bitcast(F32), xts[n][1][:].bitcast(F32))
             stv = st32.rearrange(
-                "p (s x c w g k e a) -> p x c g e s k a w", s=4, x=2, c=2, w=3, g=2, k=4, e=2, a=4)
+                "p (s x c w g k e a) -> p x c g e k s a w", s=4, x=2, c=2, w=3, g=2, k=4, e=2, a=4)
             for gg, par in parts:
                 for hp in range(2):
                     nh = 4 - hp
                     e = (par + hp + ch) % 2
                     off = (49 * e + 7 * hp + ch - par) // 2
                     src = xw[par][:, off:off + NW].rearrange(
-                        "p (g a k s r) -> p g s k a r", g=2, a=4, k=4, s=7, r=7)
-                    nc.vector.tensor_copy(out=stv[:, hp, ch, gg, e, 0:nh], in_=src[:, gg, 0:nh, :, :, 0:3])
+                        "p (g a k s r) -> p g k s a r", g=2, a=4, k=4, s=7, r=7)
+                    nc.vector.tensor_copy(out=stv[:, hp, ch, gg, e, :, 0:nh], in_=src[:, gg, :, 0:nh, :, 0:3])
 
         def transpose_x(n, ch):
             st32 = sts[n][:].bitcast(F32)

@@ -23,10 +23,10 @@ def tile_localconvolution_t_kernel(tc, x, weight, out):
     with tc.tile_pool(name="const", bufs=1) as const, \
             tc.tile_pool(name="xin", bufs=3) as xin, \
             tc.tile_pool(name="stg", bufs=2) as stg, \
-            tc.tile_pool(name="grp", bufs=2) as grp, \
+            tc.tile_pool(name="grp", bufs=3) as grp, \
             tc.tile_pool(name="cod", bufs=6) as cod, \
             tc.tile_pool(name="res", bufs=2) as res, \
-            tc.tile_pool(name="wl4", bufs=3) as wl4, \
+            tc.tile_pool(name="wl4", bufs=2) as wl4, \
             tc.tile_pool(name="wld", bufs=2) as wld, \
             tc.psum_pool(name="pt", bufs=4) as pt, \
             tc.psum_pool(name="pa", bufs=4) as pa:
@@ -130,7 +130,7 @@ def tile_localconvolution_t_kernel(tc, x, weight, out):
 
         def exit_x(n, ch):
             if ch == 0:
-                gs[n] = grp.tile([P, GW + 640], BF16, name="g", align_bytes=64)
+                gs[n] = grp.tile([P, GW + 160], BF16, name="g", align_bytes=64)
             flat = gs[n][:].bitcast(F32)
             g32 = flat[:, 0:GW // 2].rearrange("p (h j b r) -> p h j b r", h=NHB, j=COLS, b=P, r=2)
             for j in (ch, ch + 2):
@@ -147,7 +147,7 @@ def tile_localconvolution_t_kernel(tc, x, weight, out):
             flat = gs[n][:].bitcast(F32)
             g32 = flat[:, 0:GW // 2].rearrange("p (h j b r) -> p h j b r", h=NHB, j=COLS, b=P, r=2)
             lo = 2 * 2 * P + 1
-            pair = flat[:, lo:lo + 6 * 819].rearrange("p (x y) -> p y x", y=819)[:, 0:4 * P:2, 0:6:5]
+            pair = flat[:, lo:lo + 8 * 585].rearrange("p (x y) -> p y x", y=585)[:, 0:4 * P:2, 0:8:7]
             nc.vector.tensor_copy(out=g32[:, 2, 2:4], in_=pair.rearrange("p (j b) r -> p j b r", b=P))
 
         def quant_x(n, i):

@@ -22,10 +22,10 @@ def tile_localconvolution_t_kernel(tc, x, weight, out):
     nc = tc.nc
     with tc.tile_pool(name="const", bufs=1) as const, \
             tc.tile_pool(name="xin", bufs=3) as xin, \
-            tc.tile_pool(name="stg", bufs=2) as stg, \
-            tc.tile_pool(name="grp", bufs=3) as grp, \
+            tc.tile_pool(name="stg", bufs=4) as stg, \
+            tc.tile_pool(name="grp", bufs=2) as grp, \
             tc.tile_pool(name="cod", bufs=6) as cod, \
-            tc.tile_pool(name="res", bufs=2) as res, \
+            tc.tile_pool(name="res", bufs=3) as res, \
             tc.tile_pool(name="wl4", bufs=2) as wl4, \
             tc.tile_pool(name="wld", bufs=2) as wld, \
             tc.psum_pool(name="pt", bufs=4) as pt, \
@@ -34,11 +34,18 @@ def tile_localconvolution_t_kernel(tc, x, weight, out):
         make_identity(nc, ident[:])
         wc = const.tile([P, ROWS * COLS * 2 * O], U32, align_bytes=64)
         ws = const.tile([P, ROWS * COLS * 2 * O], U8, align_bytes=64)
+        all_parts = ((0, 0), (0, 1), (1, 0), (1, 1))
         xts, sts, gs, banks, codes, accs, stages = {}, {}, {}, {}, {}, {}, {}
         wraws, wsts, wgs, wbanks = {}, {}, {}, {}
 
         def col(j):
             return (j % 2) * 2 + j // 2
+
+        def warm_up():
+            dummy = pa.tile([P, COLS * O], F32, name="acc")
+            ones = ident[:].bitcast(BF16)
+            for k in range(14):
+                nc.tensor.matmul(out=dummy[:, 0:2 * P], lhsT=ones[:, 0:P], rhs=ones, start=True, stop=True)
 
         def load_x(n):
             rows = x[n * P:(n + 1) * P].rearrange("b c h w -> b (c h w)")
@@ -48,20 +55,18 @@ def tile_localconvolution_t_kernel(tc, x, weight, out):
             if n == 0:
                 for lo in range(0, 2 * NW, QUARTER):
                     nc.sync.dma_start(out=x0[:, lo:lo + QUARTER], in_=rows[:, lo:lo + QUARTER])
-                for part in (0, 2):
-                    shift_part(nc.scalar.copy, part)
             else:
                 nc.sync.dma_start(out=x0[:, 0:2 * NW], in_=rows)
                 nc.sync.dma_start(out=x1[:, 0:2 * NW - 1], in_=rows[:, 1:2 * NW])
 
-        def shift_part(copy, part):
+        def shift_part(part):
             x0, x1 = xts[0]
             lo, hi = part * QUARTER, (part + 1) * QUARTER
-            copy(out=x1[:, lo:hi - 2], in_=x0[:, lo + 1:hi - 1])
+            nc.vector.tensor_copy(out=x1[:, lo:hi - 2], in_=x0[:, lo + 1:hi - 1])
 
         def load_w(i):
             wraw = wl4.tile([P, COLS * 1024], BF16, name="wraw")
-            step = 2 if i < 2 else COLS
+            step = (2, 1, COLS, COLS)[i]
             for j in range(0, COLS, step):
                 nc.sync.dma_start(
                     out=wraw[:].rearrange("o (j k) -> o j k", j=COLS)[:, j:j + step],
@@ -103,12 +108,12 @@ def tile_localconvolution_t_kernel(tc, x, weight, out):
                 in_=wgs[i][:])
 
         def stage_x(n, ch, parts):
-            if n not in sts:
-                sts[n] = stg.tile([P, 8 * 2 * 3 * 128], BF16, name="st")
-            st32 = sts[n][:].bitcast(F32)
+            if (n, ch) not in sts:
+                sts[(n, ch)] = stg.tile([P, 8 * 3 * 128], BF16, name="st")
+            st32 = sts[(n, ch)][:].bitcast(F32)
             xw = (xts[n][0][:].bitcast(F32), xts[n][1][:].bitcast(F32))
             stv = st32.rearrange(
-                "p (s x c w g k e a) -> p x c g e k s a w", s=4, x=2, c=2, w=3, g=2, k=4, e=2, a=4)
+                "p (s x w g k e a) -> p x g e k s a w", s=4, x=2, w=3, g=2, k=4, e=2, a=4)
             for gg, par in parts:
                 for hp in range(2):
                     nh = 4 - hp
@@ -116,16 +121,16 @@ def tile_localconvolution_t_kernel(tc, x, weight, out):
                     off = (49 * e + 7 * hp + ch - par) // 2
                     src = xw[par][:, off:off + NW].rearrange(
                         "p (g a k s r) -> p g k s a r", g=2, a=4, k=4, s=7, r=7)
-                    nc.vector.tensor_copy(out=stv[:, hp, ch, gg, e, :, 0:nh], in_=src[:, gg, :, 0:nh, :, 0:3])
+                    nc.vector.tensor_copy(out=stv[:, hp, gg, e, :, 0:nh], in_=src[:, gg, :, 0:nh, :, 0:3])
 
         def transpose_x(n, ch):
-            st32 = sts[n][:].bitcast(F32)
+            st32 = sts[(n, ch)][:].bitcast(F32)
             for j in (ch, ch + 2):
                 for par in range(2):
                     pe = pt.tile([P, 4, P], F32, name="pe", tag="pt")
                     banks[(n, j, par)] = pe
                     for s, h in enumerate(range(par, H, 2)):
-                        lo = ((h * 2 + ch) * 3 + j // 2) * 64
+                        lo = (h * 3 + j // 2) * 64
                         nc.tensor.transpose(pe[:, s, :], st32[:, lo:lo + P], ident[:])
 
         def exit_x(n, ch):
@@ -137,7 +142,11 @@ def tile_localconvolution_t_kernel(tc, x, weight, out):
                 jp = col(j)
                 ev = banks[(n, j, 0)]
                 od = banks[(n, j, 1)]
-                nc.scalar.copy(out=g32[:, 0:5:4, jp], in_=ev[:].rearrange("p (h r) b -> p h b r", h=2, r=2))
+                if n == 0:
+                    for h in (0, 4):
+                        nc.scalar.copy(out=g32[:, h, jp], in_=ev[:, h // 2:h // 2 + 2, :].rearrange("p r b -> p b r"))
+                else:
+                    nc.scalar.copy(out=g32[:, 0:5:4, jp], in_=ev[:].rearrange("p (h r) b -> p h b r", h=2, r=2))
                 if jp < 2:
                     nc.scalar.copy(out=g32[:, 2, jp], in_=ev[:, 1:3, :].rearrange("p r b -> p b r"))
                 nc.scalar.copy(out=g32[:, 1, jp], in_=od[:, 0:2, :].rearrange("p r b -> p b r"))
@@ -199,68 +208,93 @@ def tile_localconvolution_t_kernel(tc, x, weight, out):
 
         def store_last(n, half):
             rows = out[n * P:(n + 1) * P].rearrange("b o i j -> b (o i j)")
-            lo, hi = half * 1024, (half + 1) * 1024
+            lo, hi = half * 512, (half + 1) * 512
             nc.sync.dma_start(out=rows[:, lo:hi], in_=stages[n][:, lo:hi])
 
-        load_x(0)
-        load_w(0)
-        load_w(1)
-        load_x(1)
-        load_w(2)
-        load_w(3)
-        load_x(2)
-        with tc.manual_schedule(engines={mybir.EngineType.DVE}):
-            shift_part(nc.vector.tensor_copy, 1)
+        with tc.manual_schedule():
+            warm_up()
+            load_x(0)
+            load_w(0)
+            load_w(1)
+            load_x(1)
+            shift_part(0)
+            shift_part(1)
             stage_x(0, 0, ((0, 0), (0, 1)))
-            shift_part(nc.vector.tensor_copy, 3)
+            shift_part(2)
+            shift_part(3)
             stage_x(0, 0, ((1, 0), (1, 1)))
-            stage_x(0, 1, ((0, 0), (0, 1), (1, 0), (1, 1)))
+            stage_x(0, 1, all_parts)
             stage_w(0)
+            load_w(2)
             stage_w(1)
-        for n in range(NBT):
-            if n + 3 < NBT:
-                load_x(n + 3)
-            for half in range(2):
-                m = n - 2 if half == 0 else n - 1
-                rows = (2, 3) if half == 0 else (0, 1)
-                if 0 <= n - 1 < NBT:
-                    quant_x(n - 1, 2 * half)
-                    quant_x(n - 1, 2 * half + 1)
-                if n < NBT:
+            load_w(3)
+            load_x(2)
+            load_x(3)
+            transpose_x(0, 0)
+            exit_x(0, 0)
+            transpose_w(0)
+            exit_w(0)
+            transpose_x(0, 1)
+            exit_x(0, 1)
+            transpose_w(1)
+            exit_w(1)
+            for i in range(ROWS):
+                quant_last(0, i, 0)
+            quant_w(0)
+            stage_x(1, 0, all_parts)
+            stage_x(1, 1, all_parts)
+            pair_x(0)
+            for i in range(2):
+                quant_last(0, i, 1)
+            stage_w(2)
+            quant_w(1)
+            stage_w(3)
+            for i in range(2, 4):
+                quant_last(0, i, 1)
+            for n in range(1, NBT):
+                if n + 3 < NBT:
+                    load_x(n + 3)
+                for half in range(2):
+                    m = n - 2 if half == 0 else n - 1
+                    rows = (2, 3) if half == 0 else (0, 1)
+                    if n == 1 and half == 1:
+                        transpose_w(3)
+                        exit_w(3)
                     transpose_x(n, half)
                     exit_x(n, half)
-                wrow = 2 * n + half
-                if wrow < ROWS:
-                    transpose_w(wrow)
-                    exit_w(wrow)
-                if 0 <= m < NBT:
-                    for i in rows:
-                        multiply(m, i)
-                    for i in rows:
-                        exit_out(m, i)
-                if wrow < ROWS:
-                    quant_w(wrow)
-                if n + 1 < NBT:
-                    stage_x(n + 1, half, ((0, 0), (0, 1), (1, 0), (1, 1)))
-                if half == 1:
-                    pair_x(n)
-                if wrow + 2 < ROWS:
-                    stage_w(wrow + 2)
-        last = NBT - 1
-        for i in (2, 3):
-            multiply(last - 1, i)
-        for i in (2, 3):
-            exit_out(last - 1, i)
-        for i in range(ROWS):
-            if i in (0, 3):
-                for half in range(2):
-                    quant_last(last, i, half)
-                    multiply(last, i, (half, half + 2))
-            else:
-                quant_x(last, i)
-                multiply(last, i)
-        for i in range(ROWS - 1):
-            exit_last(last, i, slice(0, O), nc.scalar.copy)
-        for half in range(2):
-            exit_last(last, ROWS - 1, slice(half * O // 2, (half + 1) * O // 2), nc.vector.tensor_copy)
-            store_last(last, half)
+                    if n == 1 and half == 0:
+                        transpose_w(2)
+                        exit_w(2)
+                    if n > 1:
+                        quant_x(n - 1, 2 * half)
+                        if half == 0:
+                            pair_x(n - 1)
+                    if n + 1 < NBT:
+                        stage_x(n + 1, half, all_parts)
+                    if n == 1:
+                        quant_w(half + 2)
+                    else:
+                        quant_x(n - 1, 2 * half + 1)
+                    if 0 <= m and n < NBT - 1:
+                        for i in rows:
+                            multiply(m, i)
+                        for i in rows:
+                            exit_out(m, i)
+            last = NBT - 1
+            pair_x(last)
+            for m, i in ((last - 2, 2), (last - 2, 3), (last - 1, 0), (last - 1, 1), (last - 1, 2), (last - 1, 3)):
+                multiply(m, i)
+                exit_out(m, i)
+            for i in range(ROWS):
+                if i in (0, 3):
+                    for half in range(2):
+                        quant_last(last, i, half)
+                        multiply(last, i, (half, half + 2))
+                else:
+                    quant_x(last, i)
+                    multiply(last, i)
+            for i in range(ROWS - 1):
+                exit_last(last, i, slice(0, O), nc.scalar.copy)
+            for part in range(4):
+                exit_last(last, ROWS - 1, slice(part * O // 4, (part + 1) * O // 4), nc.vector.tensor_copy)
+                store_last(last, part)

@@ -123,9 +123,9 @@ def tile_localconvolution_t_kernel(tc, x, weight, out):
                         "p (g a k s r) -> p g k s a r", g=2, a=4, k=4, s=7, r=7)
                     nc.vector.tensor_copy(out=stv[:, hp, gg, e, :, 0:nh], in_=src[:, gg, :, 0:nh, :, 0:3])
 
-        def transpose_x(n, ch):
+        def transpose_x(n, ch, js=None):
             st32 = sts[(n, ch)][:].bitcast(F32)
-            for j in (ch, ch + 2):
+            for j in js or (ch, ch + 2):
                 for par in range(2):
                     pe = pt.tile([P, 4, P], F32, name="pe", tag="pt")
                     banks[(n, j, par)] = pe
@@ -133,12 +133,12 @@ def tile_localconvolution_t_kernel(tc, x, weight, out):
                         lo = (h * 3 + j // 2) * 64
                         nc.tensor.transpose(pe[:, s, :], st32[:, lo:lo + P], ident[:])
 
-        def exit_x(n, ch):
-            if ch == 0:
+        def exit_x(n, ch, js=None):
+            if ch == 0 and n not in gs:
                 gs[n] = grp.tile([P, GW + 160], BF16, name="g", align_bytes=64)
             flat = gs[n][:].bitcast(F32)
             g32 = flat[:, 0:GW // 2].rearrange("p (h j b r) -> p h j b r", h=NHB, j=COLS, b=P, r=2)
-            for j in (ch, ch + 2):
+            for j in js or (ch, ch + 2):
                 jp = col(j)
                 ev = banks[(n, j, 0)]
                 od = banks[(n, j, 1)]
@@ -257,14 +257,24 @@ def tile_localconvolution_t_kernel(tc, x, weight, out):
                 for half in range(2):
                     m = n - 2 if half == 0 else n - 1
                     rows = (2, 3) if half == 0 else (0, 1)
-                    if n == 1 and half == 1:
-                        transpose_w(3)
-                        exit_w(3)
-                    transpose_x(n, half)
-                    exit_x(n, half)
-                    if n == 1 and half == 0:
-                        transpose_w(2)
-                        exit_w(2)
+                    if n == 1:
+                        if half == 1:
+                            transpose_w(3)
+                            exit_w(3)
+                        transpose_x(n, half)
+                        exit_x(n, half)
+                        if half == 0:
+                            transpose_w(2)
+                            exit_w(2)
+                    elif n == NBT - 1:
+                        transpose_x(n, half)
+                        exit_x(n, half)
+                    else:
+                        for k in range(2):
+                            transpose_x(n, half, (half + 2 * k,))
+                            exit_x(n, half, (half + 2 * k,))
+                            multiply(m, rows[k])
+                            exit_out(m, rows[k])
                     if n > 1:
                         quant_x(n - 1, 2 * half)
                         if half == 0:
@@ -275,7 +285,7 @@ def tile_localconvolution_t_kernel(tc, x, weight, out):
                         quant_w(half + 2)
                     else:
                         quant_x(n - 1, 2 * half + 1)
-                    if 0 <= m and n < NBT - 1:
+                    if n == 1 and half == 1:
                         for i in rows:
                             multiply(m, i)
                         for i in rows:

@@ -22,7 +22,7 @@ def tile_localconvolution_t_kernel(tc, x, weight, out):
     nc = tc.nc
     with tc.tile_pool(name="const", bufs=1) as const, \
             tc.tile_pool(name="xin", bufs=3) as xin, \
-            tc.tile_pool(name="stg", bufs=4) as stg, \
+            tc.tile_pool(name="stg", bufs=8) as stg, \
             tc.tile_pool(name="grp", bufs=2) as grp, \
             tc.tile_pool(name="cod", bufs=6) as cod, \
             tc.tile_pool(name="res", bufs=3) as res, \
@@ -38,13 +38,16 @@ def tile_localconvolution_t_kernel(tc, x, weight, out):
         xts, sts, gs, banks, codes, accs, stages = {}, {}, {}, {}, {}, {}, {}
         wraws, wsts, wgs, wbanks = {}, {}, {}, {}
 
+        def pair_columns(n):
+            return 2 if n < 4 else 3
+
         def col(j):
             return (j % 2) * 2 + j // 2
 
         def warm_up():
             dummy = pa.tile([P, COLS * O], F32, name="acc")
             ones = ident[:].bitcast(BF16)
-            for k in range(14):
+            for k in range(9):
                 nc.tensor.matmul(out=dummy[:, 0:2 * P], lhsT=ones[:, 0:P], rhs=ones, start=True, stop=True)
 
         def load_x(n):
@@ -73,12 +76,13 @@ def tile_localconvolution_t_kernel(tc, x, weight, out):
                     in_=weight[i].rearrange("j o c u v -> o j (c u v)")[:, j:j + step])
             wraws[i] = wraw
 
-        def stage_w(i):
-            wst = wld.tile([P, COLS * 1024], BF16, name="wst")
-            wsts[i] = wst
+        def stage_w(i, js=(0, 1, 2, 3)):
+            if js[0] == 0:
+                wsts[i] = wld.tile([P, COLS * 1024], BF16, name="wst")
+            wst = wsts[i]
             wraw32 = wraws[i][:].bitcast(F32)
             wst32 = wst[:].bitcast(F32)
-            for j in range(COLS):
+            for j in js:
                 wsrc = wraw32[:, j * 512:(j + 1) * 512].rearrange(
                     "p (g a b h m) -> p h g b a m", g=2, a=4, b=8, h=2, m=4)
                 wdst = wst32[:, j * 512:(j + 1) * 512].rearrange(
@@ -107,30 +111,29 @@ def tile_localconvolution_t_kernel(tc, x, weight, out):
                 scales=ws[:, i * 1024:(i + 1) * 1024],
                 in_=wgs[i][:])
 
-        def stage_x(n, ch, parts):
-            if (n, ch) not in sts:
-                sts[(n, ch)] = stg.tile([P, 8 * 3 * 128], BF16, name="st")
-            st32 = sts[(n, ch)][:].bitcast(F32)
+        def stage_x(n, ch, parts, hps=(0, 1)):
             xw = (xts[n][0][:].bitcast(F32), xts[n][1][:].bitcast(F32))
-            stv = st32.rearrange(
-                "p (s x w g k e a) -> p x g e k s a w", s=4, x=2, w=3, g=2, k=4, e=2, a=4)
             for gg, par in parts:
-                for hp in range(2):
+                for hp in hps:
+                    if (n, ch, hp) not in sts:
+                        sts[(n, ch, hp)] = stg.tile([P, 4 * 3 * 128], BF16, name="st")
+                    stv = sts[(n, ch, hp)][:].bitcast(F32).rearrange(
+                        "p (s w g k e a) -> p g e k s a w", s=4, w=3, g=2, k=4, e=2, a=4)
                     nh = 4 - hp
                     e = (par + hp + ch) % 2
                     off = (49 * e + 7 * hp + ch - par) // 2
                     src = xw[par][:, off:off + NW].rearrange(
                         "p (g a k s r) -> p g k s a r", g=2, a=4, k=4, s=7, r=7)
-                    nc.vector.tensor_copy(out=stv[:, hp, gg, e, :, 0:nh], in_=src[:, gg, :, 0:nh, :, 0:3])
+                    nc.vector.tensor_copy(out=stv[:, gg, e, :, 0:nh], in_=src[:, gg, :, 0:nh, :, 0:3])
 
         def transpose_x(n, ch, js=None):
-            st32 = sts[(n, ch)][:].bitcast(F32)
-            for j in js or (ch, ch + 2):
-                for par in range(2):
+            for par in range(2):
+                st32 = sts[(n, ch, par)][:].bitcast(F32)
+                for j in js or (ch, ch + 2):
                     pe = pt.tile([P, 4, P], F32, name="pe", tag="pt")
                     banks[(n, j, par)] = pe
                     for s, h in enumerate(range(par, H, 2)):
-                        lo = (h * 3 + j // 2) * 64
+                        lo = (s * 3 + j // 2) * 64
                         nc.tensor.transpose(pe[:, s, :], st32[:, lo:lo + P], ident[:])
 
         def exit_x(n, ch, js=None):
@@ -141,23 +144,27 @@ def tile_localconvolution_t_kernel(tc, x, weight, out):
             for j in js or (ch, ch + 2):
                 jp = col(j)
                 ev = banks[(n, j, 0)]
-                od = banks[(n, j, 1)]
                 if n == 0:
                     for h in (0, 4):
                         nc.scalar.copy(out=g32[:, h, jp], in_=ev[:, h // 2:h // 2 + 2, :].rearrange("p r b -> p b r"))
                 else:
                     nc.scalar.copy(out=g32[:, 0:5:4, jp], in_=ev[:].rearrange("p (h r) b -> p h b r", h=2, r=2))
-                if jp < 2:
+                if jp < 4 - pair_columns(n):
                     nc.scalar.copy(out=g32[:, 2, jp], in_=ev[:, 1:3, :].rearrange("p r b -> p b r"))
+            for j in js or (ch, ch + 2):
+                jp = col(j)
+                od = banks[(n, j, 1)]
                 nc.scalar.copy(out=g32[:, 1, jp], in_=od[:, 0:2, :].rearrange("p r b -> p b r"))
                 nc.scalar.copy(out=g32[:, 3, jp], in_=od[:, 1:3, :].rearrange("p r b -> p b r"))
 
         def pair_x(n):
             flat = gs[n][:].bitcast(F32)
             g32 = flat[:, 0:GW // 2].rearrange("p (h j b r) -> p h j b r", h=NHB, j=COLS, b=P, r=2)
-            lo = 2 * 2 * P + 1
-            pair = flat[:, lo:lo + 8 * 585].rearrange("p (x y) -> p y x", y=585)[:, 0:4 * P:2, 0:8:7]
-            nc.vector.tensor_copy(out=g32[:, 2, 2:4], in_=pair.rearrange("p (j b) r -> p j b r", b=P))
+            num = pair_columns(n)
+            lo = (4 - num) * 2 * P + 1
+            steps = (15, 7, 5)[num - 1]
+            pair = flat[:, lo:lo + (steps + 1) * (4095 // steps)].rearrange("p (x y) -> p y x", x=steps + 1)[:, 0:num * 2 * P:2, 0:steps + 1:steps]
+            nc.vector.tensor_copy(out=g32[:, 2, 4 - num:4], in_=pair.rearrange("p (j b) r -> p j b r", b=P))
 
         def quant_x(n, i):
             pc = cod.tile([P, 1024], U32, name="pc", align_bytes=64)
@@ -219,27 +226,31 @@ def tile_localconvolution_t_kernel(tc, x, weight, out):
             load_x(1)
             shift_part(0)
             shift_part(1)
-            stage_x(0, 0, ((0, 0), (0, 1)))
+            stage_x(0, 0, ((0, 0), (0, 1)), (0,))
+            stage_x(0, 0, ((0, 0),), (1,))
             shift_part(2)
             shift_part(3)
-            stage_x(0, 0, ((1, 0), (1, 1)))
+            stage_x(0, 0, ((1, 0), (1, 1)), (0,))
+            stage_x(0, 0, ((0, 1), (1, 0), (1, 1)), (1,))
             stage_x(0, 1, all_parts)
             stage_w(0)
             load_w(2)
-            stage_w(1)
-            load_w(3)
-            load_x(2)
-            load_x(3)
+            stage_w(1, (0, 1, 2))
             transpose_x(0, 0)
             exit_x(0, 0)
             transpose_w(0)
             exit_w(0)
             transpose_x(0, 1)
             exit_x(0, 1)
-            transpose_w(1)
-            exit_w(1)
             for i in range(ROWS):
                 quant_last(0, i, 0)
+                if i == 0:
+                    stage_w(1, (3,))
+                    load_w(3)
+                    load_x(2)
+                    load_x(3)
+            transpose_w(1)
+            exit_w(1)
             quant_w(0)
             stage_x(1, 0, all_parts)
             stage_x(1, 1, all_parts)
@@ -279,10 +290,13 @@ def tile_localconvolution_t_kernel(tc, x, weight, out):
                         quant_x(n - 1, 2 * half)
                         if half == 0:
                             pair_x(n - 1)
+                    if n == 1 and half == 0:
+                        quant_w(2)
                     if n + 1 < NBT:
                         stage_x(n + 1, half, all_parts)
                     if n == 1:
-                        quant_w(half + 2)
+                        if half == 1:
+                            quant_w(3)
                     else:
                         quant_x(n - 1, 2 * half + 1)
                     if n == 1 and half == 1:

@@ -39,7 +39,7 @@ def tile_localconvolution_t_kernel(tc, x, weight, out):
         wraws, wsts, wgs, wbanks = {}, {}, {}, {}
 
         def pair_columns(n):
-            return 2 if n < 4 else 3
+            return (3 if n > 1 else 2) if n < NBT - 1 else 0
 
         def col(j):
             return (j % 2) * 2 + j // 2
@@ -149,13 +149,16 @@ def tile_localconvolution_t_kernel(tc, x, weight, out):
                         nc.scalar.copy(out=g32[:, h, jp], in_=ev[:, h // 2:h // 2 + 2, :].rearrange("p r b -> p b r"))
                 else:
                     nc.scalar.copy(out=g32[:, 0:5:4, jp], in_=ev[:].rearrange("p (h r) b -> p h b r", h=2, r=2))
-                if jp < 4 - pair_columns(n):
+                if jp < 4 - pair_columns(n) and (n < NBT - 1 or ch == 0):
                     nc.scalar.copy(out=g32[:, 2, jp], in_=ev[:, 1:3, :].rearrange("p r b -> p b r"))
             for j in js or (ch, ch + 2):
                 jp = col(j)
                 od = banks[(n, j, 1)]
                 nc.scalar.copy(out=g32[:, 1, jp], in_=od[:, 0:2, :].rearrange("p r b -> p b r"))
                 nc.scalar.copy(out=g32[:, 3, jp], in_=od[:, 1:3, :].rearrange("p r b -> p b r"))
+            if n == NBT - 1 and ch == 1:
+                for j in (1, 3):
+                    nc.scalar.copy(out=g32[:, 2, col(j)], in_=banks[(n, j, 0)][:, 1:3, :].rearrange("p r b -> p b r"))
 
         def pair_x(n):
             flat = gs[n][:].bitcast(F32)
@@ -287,13 +290,15 @@ def tile_localconvolution_t_kernel(tc, x, weight, out):
                             multiply(m, rows[k])
                             exit_out(m, rows[k])
                     if n > 1:
-                        quant_x(n - 1, 2 * half)
+                        if n + 1 < NBT:
+                            stage_x(n + 1, half, all_parts)
                         if half == 0:
                             pair_x(n - 1)
+                        quant_x(n - 1, 2 * half)
                     if n == 1 and half == 0:
                         quant_w(2)
                     if n + 1 < NBT:
-                        stage_x(n + 1, half, all_parts)
+                        stage_x(n + 1, half, all_parts if n == 1 else ())
                     if n == 1:
                         if half == 1:
                             quant_w(3)
@@ -305,20 +310,19 @@ def tile_localconvolution_t_kernel(tc, x, weight, out):
                         for i in rows:
                             exit_out(m, i)
             last = NBT - 1
-            pair_x(last)
             for m, i in ((last - 2, 2), (last - 2, 3), (last - 1, 0), (last - 1, 1), (last - 1, 2), (last - 1, 3)):
                 multiply(m, i)
                 exit_out(m, i)
             for i in range(ROWS):
-                if i in (0, 3):
+                if i < ROWS - 1:
+                    quant_x(last, i)
+                    multiply(last, i)
+                else:
                     for half in range(2):
                         quant_last(last, i, half)
                         multiply(last, i, (half, half + 2))
-                else:
-                    quant_x(last, i)
-                    multiply(last, i)
             for i in range(ROWS - 1):
                 exit_last(last, i, slice(0, O), nc.scalar.copy)
             for part in range(4):
-                exit_last(last, ROWS - 1, slice(part * O // 4, (part + 1) * O // 4), nc.vector.tensor_copy)
+                exit_last(last, ROWS - 1, slice(part * O // 4, (part + 1) * O // 4), nc.scalar.copy)
                 store_last(last, part)

import concourse.mybir as mybir
from concourse.masks import make_identity

F32 = mybir.dt.float32
BF16 = mybir.dt.bfloat16
U32 = mybir.dt.uint32
U8 = mybir.dt.uint8
FP8X4 = mybir.dt.float8_e4m3fn_x4

P = 128
B, C, O, ROWS, COLS, KH, KW, H, W = 1024, 64, 128, 4, 4, 4, 4, 7, 7
FLOPS = 2 * ROWS * COLS * B * O * C * KH * KW
NBT = B // P
NHB = 5
GW = NHB * COLS * P * 4
XPAD = 3200
QUARTER = C * H * W // 4
NW = C * H * W // 2


def tile_localconvolution_t_kernel(tc, x, weight, out):
    nc = tc.nc
    with tc.tile_pool(name="const", bufs=1) as const, \
            tc.tile_pool(name="xin", bufs=3) as xin, \
            tc.tile_pool(name="stg", bufs=8) as stg, \
            tc.tile_pool(name="grp", bufs=2) as grp, \
            tc.tile_pool(name="cod", bufs=6) as cod, \
            tc.tile_pool(name="res", bufs=3) as res, \
            tc.tile_pool(name="wl4", bufs=2) as wl4, \
            tc.tile_pool(name="wld", bufs=2) as wld, \
            tc.psum_pool(name="pt", bufs=4) as pt, \
            tc.psum_pool(name="pa", bufs=4) as pa:
        ident = const.tile([P, P], F32)
        make_identity(nc, ident[:])
        wc = const.tile([P, ROWS * COLS * 2 * O], U32, align_bytes=64)
        ws = const.tile([P, ROWS * COLS * 2 * O], U8, align_bytes=64)
        all_parts = ((0, 0), (0, 1), (1, 0), (1, 1))
        xts, sts, gs, banks, codes, accs, stages = {}, {}, {}, {}, {}, {}, {}
        wraws, wsts, wgs, wbanks = {}, {}, {}, {}

        def pair_columns(n):
            return (3 if n > 1 else 2) if n < NBT - 1 else 0

        def col(j):
            return (j % 2) * 2 + j // 2

        def warm_up():
            dummy = pa.tile([P, COLS * O], F32, name="acc")
            ones = ident[:].bitcast(BF16)
            for k in range(9):
                nc.tensor.matmul(out=dummy[:, 0:2 * P], lhsT=ones[:, 0:P], rhs=ones, start=True, stop=True)

        def load_x(n):
            rows = x[n * P:(n + 1) * P].rearrange("b c h w -> b (c h w)")
            x0 = xin.tile([P, XPAD], BF16, name="x0")
            x1 = xin.tile([P, XPAD], BF16, name="x1")
            xts[n] = (x0, x1)
            if n == 0:
                for lo in range(0, 2 * NW, QUARTER):
                    nc.sync.dma_start(out=x0[:, lo:lo + QUARTER], in_=rows[:, lo:lo + QUARTER])
            else:
                nc.sync.dma_start(out=x0[:, 0:2 * NW], in_=rows)
                nc.sync.dma_start(out=x1[:, 0:2 * NW - 1], in_=rows[:, 1:2 * NW])

        def shift_part(part):
            x0, x1 = xts[0]
            lo, hi = part * QUARTER, (part + 1) * QUARTER
            nc.vector.tensor_copy(out=x1[:, lo:hi - 2], in_=x0[:, lo + 1:hi - 1])

        def load_w(i):
            wraw = wl4.tile([P, COLS * 1024], BF16, name="wraw")
            step = (2, 1, COLS, COLS)[i]
            for j in range(0, COLS, step):
                nc.sync.dma_start(
                    out=wraw[:].rearrange("o (j k) -> o j k", j=COLS)[:, j:j + step],
                    in_=weight[i].rearrange("j o c u v -> o j (c u v)")[:, j:j + step])
            wraws[i] = wraw

        def stage_w(i, js=(0, 1, 2, 3)):
            if js[0] == 0:
                wsts[i] = wld.tile([P, COLS * 1024], BF16, name="wst")
            wst = wsts[i]
            wraw32 = wraws[i][:].bitcast(F32)
            wst32 = wst[:].bitcast(F32)
            for j in js:
                wsrc = wraw32[:, j * 512:(j + 1) * 512].rearrange(
                    "p (g a b h m) -> p h g b a m", g=2, a=4, b=8, h=2, m=4)
                wdst = wst32[:, j * 512:(j + 1) * 512].rearrange(
                    "p (h m g b a) -> p h g b a m", h=2, m=4, g=2, b=8, a=4)
                for uh in range(2):
                    nc.vector.tensor_copy(out=wdst[:, uh], in_=wsrc[:, uh])

        def transpose_w(i):
            wst32 = wsts[i][:].bitcast(F32)
            for j in range(COLS):
                pw = pt.tile([P, 4, P], F32, name="pw", tag="pt")
                wbanks[(i, j)] = pw
                for u in range(KH):
                    nc.tensor.transpose(pw[:, u, :], wst32[:, (j * 4 + u) * P:(j * 4 + u + 1) * P], ident[:])

        def exit_w(i):
            wg = wld.tile([P, COLS * 1024], BF16, name="wg", align_bytes=64)
            wgs[i] = wg
            wg32 = wg[:].bitcast(F32).rearrange("p (j q o r) -> p j q o r", j=COLS, q=2, o=O, r=2)
            for j in range(COLS):
                nc.scalar.copy(out=wg32[:, j], in_=wbanks[(i, j)][:].rearrange("p (r q) o -> p q o r", r=2, q=2))

        def quant_w(i):
            nc.vector.quantize_mx(
                out=wc[:, i * 1024:(i + 1) * 1024].bitcast(FP8X4),
                scales=ws[:, i * 1024:(i + 1) * 1024],
                in_=wgs[i][:])

        def stage_x(n, ch, parts, hps=(0, 1)):
            xw = (xts[n][0][:].bitcast(F32), xts[n][1][:].bitcast(F32))
            for gg, par in parts:
                for hp in hps:
                    if (n, ch, hp) not in sts:
                        sts[(n, ch, hp)] = stg.tile([P, 4 * 3 * 128], BF16, name="st")
                    stv = sts[(n, ch, hp)][:].bitcast(F32).rearrange(
                        "p (s w g k e a) -> p g e k s a w", s=4, w=3, g=2, k=4, e=2, a=4)
                    nh = 4 - hp
                    e = (par + hp + ch) % 2
                    off = (49 * e + 7 * hp + ch - par) // 2
                    src = xw[par][:, off:off + NW].rearrange(
                        "p (g a k s r) -> p g k s a r", g=2, a=4, k=4, s=7, r=7)
                    nc.vector.tensor_copy(out=stv[:, gg, e, :, 0:nh], in_=src[:, gg, :, 0:nh, :, 0:3])

        def transpose_x(n, ch, js=None):
            for par in range(2):
                st32 = sts[(n, ch, par)][:].bitcast(F32)
                for j in js or (ch, ch + 2):
                    pe = pt.tile([P, 4, P], F32, name="pe", tag="pt")
                    banks[(n, j, par)] = pe
                    for s, h in enumerate(range(par, H, 2)):
                        lo = (s * 3 + j // 2) * 64
                        nc.tensor.transpose(pe[:, s, :], st32[:, lo:lo + P], ident[:])

        def exit_x(n, ch, js=None):
            if ch == 0 and n not in gs:
                gs[n] = grp.tile([P, GW + 160], BF16, name="g", align_bytes=64)
            flat = gs[n][:].bitcast(F32)
            g32 = flat[:, 0:GW // 2].rearrange("p (h j b r) -> p h j b r", h=NHB, j=COLS, b=P, r=2)
            for j in js or (ch, ch + 2):
                jp = col(j)
                ev = banks[(n, j, 0)]
                if n == 0:
                    for h in (0, 4):
                        nc.scalar.copy(out=g32[:, h, jp], in_=ev[:, h // 2:h // 2 + 2, :].rearrange("p r b -> p b r"))
                else:
                    nc.scalar.copy(out=g32[:, 0:5:4, jp], in_=ev[:].rearrange("p (h r) b -> p h b r", h=2, r=2))
                if jp < 4 - pair_columns(n) and (n < NBT - 1 or ch == 0):
                    nc.scalar.copy(out=g32[:, 2, jp], in_=ev[:, 1:3, :].rearrange("p r b -> p b r"))
            for j in js or (ch, ch + 2):
                jp = col(j)
                od = banks[(n, j, 1)]
                nc.scalar.copy(out=g32[:, 1, jp], in_=od[:, 0:2, :].rearrange("p r b -> p b r"))
                nc.scalar.copy(out=g32[:, 3, jp], in_=od[:, 1:3, :].rearrange("p r b -> p b r"))
            if n == NBT - 1 and ch == 1:
                for j in (1, 3):
                    nc.scalar.copy(out=g32[:, 2, col(j)], in_=banks[(n, j, 0)][:, 1:3, :].rearrange("p r b -> p b r"))

        def pair_x(n):
            flat = gs[n][:].bitcast(F32)
            g32 = flat[:, 0:GW // 2].rearrange("p (h j b r) -> p h j b r", h=NHB, j=COLS, b=P, r=2)
            num = pair_columns(n)
            lo = (4 - num) * 2 * P + 1
            steps = (15, 7, 5)[num - 1]
            pair = flat[:, lo:lo + (steps + 1) * (4095 // steps)].rearrange("p (x y) -> p y x", x=steps + 1)[:, 0:num * 2 * P:2, 0:steps + 1:steps]
            nc.vector.tensor_copy(out=g32[:, 2, 4 - num:4], in_=pair.rearrange("p (j b) r -> p j b r", b=P))

        def quant_x(n, i):
            pc = cod.tile([P, 1024], U32, name="pc", align_bytes=64)
            psc = cod.tile([P, 1024], U8, name="psc", align_bytes=64)
            codes[(n, i)] = (pc, psc)
            nc.vector.quantize_mx(out=pc[:].bitcast(FP8X4), scales=psc[:], in_=gs[n][:, i * 2048:i * 2048 + 4096])

        def multiply(n, i, js=(0, 1, 2, 3)):
            pc, psc = codes[(n, i)]
            if js[0] == 0:
                accs[(n, i)] = pa.tile([P, COLS * O], F32, name="acc")
            acc = accs[(n, i)]
            for j in js:
                for q in range(2):
                    lo = q * 512 + col(j) * P
                    wo = ((i * COLS + j) * 2 + q) * O
                    nc.tensor.matmul_mx(
                        out=acc[:, j * O:(j + 1) * O],
                        lhsT=pc[:, lo:lo + P].bitcast(FP8X4), lhsT_scale=psc[:, lo:lo + P],
                        rhs=wc[:, wo:wo + O].bitcast(FP8X4), rhs_scale=ws[:, wo:wo + O],
                        start=(q == 0), stop=(q == 1))

        def quant_last(n, i, half):
            if half == 0:
                pc = cod.tile([P, 1024], U32, name="pc", align_bytes=64)
                psc = cod.tile([P, 1024], U8, name="psc", align_bytes=64)
                codes[(n, i)] = (pc, psc)
            pc, psc = codes[(n, i)]
            for q in range(2):
                lo = q * 512 + half * 2 * P
                src = ((i + q) * COLS + half * 2) * 512
                nc.vector.quantize_mx(out=pc[:, lo:lo + 2 * P].bitcast(FP8X4), scales=psc[:, lo:lo + 2 * P],
                                      in_=gs[n][:, src:src + 1024])

        def exit_out(n, i):
            if i == 0:
                stages[n] = res.tile([P, O * ROWS * COLS], F32, name="stage")
            sgv = stages[n][:].rearrange("p (o i j) -> p o i j", o=O, i=ROWS, j=COLS)
            nc.scalar.copy(out=sgv[:, :, i, :], in_=accs[(n, i)][:].rearrange("p (j o) -> p o j", j=COLS))
            if i == ROWS - 1:
                nc.sync.dma_start(out=out[n * P:(n + 1) * P].rearrange("b o i j -> b (o i j)"), in_=stages[n][:])

        def exit_last(n, i, span, eng):
            if i == 0:
                stages[n] = res.tile([P, O * ROWS * COLS], F32, name="stage")
            sgv = stages[n][:].rearrange("p (o i j) -> p o i j", o=O, i=ROWS, j=COLS)
            eng(out=sgv[:, span, i, :], in_=accs[(n, i)][:].rearrange("p (j o) -> p o j", j=COLS)[:, span])

        def store_last(n, half):
            rows = out[n * P:(n + 1) * P].rearrange("b o i j -> b (o i j)")
            lo, hi = half * 512, (half + 1) * 512
            nc.sync.dma_start(out=rows[:, lo:hi], in_=stages[n][:, lo:hi])

        with tc.manual_schedule():
            warm_up()
            load_x(0)
            load_w(0)
            load_w(1)
            load_x(1)
            shift_part(0)
            shift_part(1)
            stage_x(0, 0, ((0, 0), (0, 1)), (0,))
            stage_x(0, 0, ((0, 0),), (1,))
            shift_part(2)
            shift_part(3)
            stage_x(0, 0, ((1, 0), (1, 1)), (0,))
            stage_x(0, 0, ((0, 1), (1, 0), (1, 1)), (1,))
            stage_x(0, 1, all_parts)
            stage_w(0)
            load_w(2)
            stage_w(1, (0, 1, 2))
            transpose_x(0, 0)
            exit_x(0, 0)
            transpose_w(0)
            exit_w(0)
            transpose_x(0, 1)
            exit_x(0, 1)
            for i in range(ROWS):
                quant_last(0, i, 0)
                if i == 0:
                    stage_w(1, (3,))
                    load_w(3)
                    load_x(2)
                    load_x(3)
            transpose_w(1)
            exit_w(1)
            quant_w(0)
            stage_x(1, 0, all_parts)
            stage_x(1, 1, all_parts)
            pair_x(0)
            for i in range(2):
                quant_last(0, i, 1)
            stage_w(2)
            quant_w(1)
            stage_w(3)
            for i in range(2, 4):
                quant_last(0, i, 1)
            for n in range(1, NBT):
                if n + 3 < NBT:
                    load_x(n + 3)
                for half in range(2):
                    m = n - 2 if half == 0 else n - 1
                    rows = (2, 3) if half == 0 else (0, 1)
                    if n == 1:
                        if half == 1:
                            transpose_w(3)
                            exit_w(3)
                        transpose_x(n, half)
                        exit_x(n, half)
                        if half == 0:
                            transpose_w(2)
                            exit_w(2)
                    elif n == NBT - 1:
                        transpose_x(n, half)
                        exit_x(n, half)
                    else:
                        for k in range(2):
                            transpose_x(n, half, (half + 2 * k,))
                            exit_x(n, half, (half + 2 * k,))
                            multiply(m, rows[k])
                            exit_out(m, rows[k])
                    if n > 1:
                        if n + 1 < NBT:
                            stage_x(n + 1, half, all_parts)
                        if half == 0:
                            pair_x(n - 1)
                        quant_x(n - 1, 2 * half)
                    if n == 1 and half == 0:
                        quant_w(2)
                    if n + 1 < NBT:
                        stage_x(n + 1, half, all_parts if n == 1 else ())
                    if n == 1:
                        if half == 1:
                            quant_w(3)
                    else:
                        quant_x(n - 1, 2 * half + 1)
                    if n == 1 and half == 1:
                        for i in rows:
                            multiply(m, i)
                        for i in rows:
                            exit_out(m, i)
            last = NBT - 1
            for m, i in ((last - 2, 2), (last - 2, 3), (last - 1, 0), (last - 1, 1), (last - 1, 2), (last - 1, 3)):
                multiply(m, i)
                exit_out(m, i)
            for i in range(ROWS):
                if i < ROWS - 1:
                    quant_x(last, i)
                    multiply(last, i)
                else:
                    for half in range(2):
                        quant_last(last, i, half)
                        multiply(last, i, (half, half + 2))
            for i in range(ROWS - 1):
                exit_last(last, i, slice(0, O), nc.scalar.copy)
            for part in range(4):
                exit_last(last, ROWS - 1, slice(part * O // 4, (part + 1) * O // 4), nc.scalar.copy)
                store_last(last, part)
